import numpy as np
import ml_dtypes


def mxq(x, axis, fmt="e4m3"):
    dtype, down = {"e4m3": (ml_dtypes.float8_e4m3fn, 7), "e5m2": (ml_dtypes.float8_e5m2, 14)}[fmt]
    v = np.moveaxis(np.asarray(x, np.float32).astype(ml_dtypes.bfloat16).astype(np.float64), axis, -1)
    blocks = v.reshape(v.shape[:-1] + (-1, 32))
    amax = np.abs(blocks).max(-1, keepdims=True)
    byte = np.maximum(np.where(amax > 0, np.frexp(amax)[1] - 1 + 127, 0) - down, 1)
    scale = np.exp2(byte - 127.0)
    codes = (blocks / scale).astype(np.float32).astype(dtype).astype(np.float64)
    return np.moveaxis((codes * scale).reshape(v.shape), -1, axis)


WIDE = False


def mx_kscale(k):
    if not WIDE:
        return np.ones(k)
    levels = np.array([10, -10, 5, -5, 0])
    a = np.random.permutation(np.resize(levels, k // 512 * 4)).reshape(k // 512, 4)
    idx = np.arange(k)
    return np.exp2(a[idx // 512, idx % 128 // 32])


BF16 = ml_dtypes.bfloat16


def bf(x):
    return np.asarray(x, np.float32).astype(BF16)


def f64(x):
    return np.asarray(x).astype(np.float64)


N, D, O, KD = 16384, 64, 256, 8
BLK = 32


def cheby(t, kd):
    T = [np.ones_like(t), t]
    for _ in range(2, kd):
        T.append(2.0 * t * T[-1] - T[-2])
    return np.stack(T[:kd], axis=-1)


def setup_inputs():
    s = mx_kscale(D * KD)
    h = np.repeat(np.maximum(s.reshape(-1, BLK)[:, 0], 1.0), BLK // KD)
    x = np.random.standard_normal((N, D)) / h[None, :] ** 4
    c = np.random.standard_normal((O, D, KD)) / np.sqrt(D * KD)
    c[:, :, 1::2] *= h[None, :, None] ** 2
    c[:, :, 0::2] /= h[None, :, None] ** 2
    return {"x": bf(x),
            "cheby_coeffs": bf(c),
            "bias": bf(np.random.standard_normal((1, O)) * 0.2)}


def reference(x, cheby_coeffs, bias):
    xt = np.tanh(f64(x))
    T = cheby(xt, KD)
    Tf = T.reshape(N, D * KD)
    W = f64(cheby_coeffs).reshape(O, D * KD)
    y = mxq(Tf, 1, "e4m3") @ mxq(W, 1, "e4m3").T
    return y + f64(bias)

@@ -1,0 +1,203 @@
+from contextlib import ExitStack
+
+import concourse.mybir as mybir
+from concourse.masks import make_identity
+
+F32 = mybir.dt.float32
+BF16 = mybir.dt.bfloat16
+U32 = mybir.dt.uint32
+U8 = mybir.dt.uint8
+FP8X4 = mybir.dt.float8_e4m3fn_x4
+ACT = mybir.ActivationFunctionType
+ALU = mybir.AluOpType
+
+P = 128
+N_ROWS, D_IN, N_OUT, N_DEG = 16384, 64, 256, 8
+K_ALL = D_IN * N_DEG
+FLOPS = 2 * N_ROWS * K_ALL * N_OUT
+
+NB = N_ROWS // P
+UNIT = 8
+N_UNITS = NB // UNIT
+X_CHUNKS = (1, 3, 4, 8)
+TT_BUFS = 3
+VEC_EVAC = ((3, 7), (7,))
+
+
+def tile_cfkanlayer_t_kernel(tc, x, cheby_coeffs, bias, out):
+    nc = tc.nc
+    with ExitStack() as ctx:
+        const = ctx.enter_context(tc.tile_pool(name="const", bufs=1))
+        work = ctx.enter_context(tc.tile_pool(name="work", bufs=3))
+        outp = ctx.enter_context(tc.tile_pool(name="outp", bufs=4))
+        tps = ctx.enter_context(tc.psum_pool(name="tps", bufs=5))
+        ops = ctx.enter_context(tc.psum_pool(name="ops", bufs=3))
+
+        x_rows = x.rearrange("(p t) d -> p (t d)", t=NB)
+        x_tiles = []
+        unit_src = []
+        first = 0
+        for ci, n_units in enumerate(X_CHUNKS):
+            width = n_units * UNIT * D_IN
+            xt = const.tile([P, width], BF16, name="x%d" % ci)
+            nc.sync.dma_start(out=xt[:], in_=x_rows[:, first * UNIT * D_IN : first * UNIT * D_IN + width])
+            x_tiles.append(xt)
+            for j in range(n_units):
+                unit_src.append((ci, j))
+            first += n_units
+
+        w_raw = const.tile([P, 2, K_ALL], BF16, name="w_raw")
+        nc.scalar.dma_start(out=w_raw[:], in_=cheby_coeffs.rearrange("(h p) d k -> p h (d k)", p=P))
+        bias_bf = const.tile([P, N_OUT], BF16, name="bias_bf")
+        nc.gpsimd.dma_start(out=bias_bf[:], in_=bias.rearrange("o n -> (o n)").partition_broadcast(P))
+
+        ident = const.tile([P, P], F32, name="ident")
+        make_identity(nc, ident[:])
+
+        shifts = const.tile([P, 3], F32, name="shifts")
+        nc.vector.memset(shifts[:, 0:1], -2.0)
+        nc.vector.memset(shifts[:, 1:2], -2.5)
+        nc.vector.memset(shifts[:, 2:3], 1.0)
+
+        pat = const.tile([P, P], F32, name="pat")
+        pat_v = pat[:].rearrange("p (c k i) -> p c k i", c=4, k=N_DEG, i=4)
+        nc.vector.memset(pat[0:64, :], 1.0)
+        nc.vector.memset(pat_v[0:64, :, 2, :], 0.5)
+        nc.vector.memset(pat_v[0:64, :, 4, :], 0.5)
+        nc.vector.memset(pat_v[0:64, :, 6, :], 2.0)
+        nc.vector.memset(pat[64:128, :], 0.0)
+        nc.vector.memset(pat_v[64:128, :, 2, :], -1.0)
+        nc.vector.memset(pat_v[64:128, :, 4, :], -1.0)
+        nc.vector.memset(pat_v[64:128, :, 6, :], -1.0)
+        pat_ps = tps.tile([P, 4 * P], F32, name="pat_ps", tag="tp")
+        nc.tensor.transpose(out=pat_ps[:, 0:P], in_=pat[:], identity=ident[:])
+        fac = const.tile([P, 1], F32, name="fac")
+        add = const.tile([P, 1], F32, name="add")
+        nc.vector.tensor_copy(out=fac[:], in_=pat_ps[:, 0:1])
+        nc.vector.tensor_copy(out=add[:], in_=pat_ps[:, 64:65])
+
+        bias_f = const.tile([P, 2, N_OUT], F32, name="bias_f")
+        nc.vector.tensor_copy(out=bias_f[:, 0, :], in_=bias_bf[:])
+        nc.vector.tensor_copy(out=bias_f[:, 1, :], in_=bias_bf[:])
+
+        w_f = const.tile([P, 2 * K_ALL], F32, name="w_f")
+        nc.vector.tensor_copy(
+            out=w_f[:].rearrange("p (g k i) -> p g k i", k=N_DEG, i=4),
+            in_=w_raw[:].rearrange("p h (g i k) -> p (h g) k i", i=4, k=N_DEG),
+        )
+        w_grp = const.tile([P, N_OUT, 4], BF16, name="w_grp", align_bytes=64)
+        for h in range(2):
+            w_ps = tps.tile([P, 4 * P], F32, name="w_ps", tag="tp")
+            for a in range(4):
+                nc.tensor.transpose(
+                    out=w_ps[:, a * P : (a + 1) * P],
+                    in_=w_f[:, (h * 4 + a) * P : (h * 4 + a + 1) * P],
+                    identity=ident[:],
+                )
+            nc.vector.tensor_copy(
+                out=w_grp[:, h * P : (h + 1) * P, :],
+                in_=w_ps[:].rearrange("p (a o) -> p o a", a=4),
+            )
+        w_codes = const.tile([P, N_OUT], U32, name="w_codes", align_bytes=64)
+        w_scales = const.tile([P, N_OUT], U8, name="w_scales", align_bytes=64)
+        nc.vector.quantize_mx(
+            out=w_codes[:].bitcast(FP8X4),
+            scales=w_scales[:],
+            in_=w_grp[:].rearrange("p o a -> p (o a)"),
+        )
+
+        tts = []
+        for b in range(TT_BUFS):
+            tt = const.tile([P, UNIT * K_ALL], F32, name="tt%d" % b)
+            tts.append(tt)
+            nc.scalar.activation(
+                out=tt[:].rearrange("p (x k i) -> p x k i", k=N_DEG, i=4)[:, :, 0, :],
+                in_=shifts[:, 2:3].unsqueeze(2).to_broadcast([P, UNIT * D_IN // 4, 4]),
+                func=ACT.Identity,
+            )
+
+        grouped = {}
+        codes = {}
+        scales = {}
+        out_rows = out.rearrange("(p t) o -> p t o", t=NB)
+
+        def gen(u):
+            ci, j = unit_src[u]
+            xs = x_tiles[ci][:, j * UNIT * D_IN : (j + 1) * UNIT * D_IN].rearrange("p (x i) -> p x i", i=4)
+            tv = tts[u % TT_BUFS][:].rearrange("p (x k i) -> p x k i", k=N_DEG, i=4)
+            t1 = tv[:, :, 1, :]
+            s4 = tv[:, :, 2, :]
+            t3 = tv[:, :, 3, :]
+            q = tv[:, :, 4, :]
+            sq5 = work.tile([P, UNIT * D_IN], F32, name="sq5")
+            p7 = work.tile([P, UNIT * D_IN], F32, name="p7")
+            sq5v = sq5[:].rearrange("p (x i) -> p x i", i=4)
+            p7v = p7[:].rearrange("p (x i) -> p x i", i=4)
+            nc.scalar.activation(out=t1, in_=xs, func=ACT.Tanh)
+            nc.scalar.activation(out=s4, in_=t1, func=ACT.Square, scale=2.0)
+            nc.vector.scalar_tensor_tensor(out=t3, in0=s4, scalar=3.0, in1=t1, op0=ALU.subtract, op1=ALU.mult)
+            nc.scalar.activation(out=q, in_=s4, func=ACT.Square, bias=shifts[:, 0:1])
+            nc.scalar.activation(out=sq5v, in_=s4, func=ACT.Square, bias=shifts[:, 1:2])
+            nc.gpsimd.tensor_tensor(out=tv[:, :, 6, :], in0=t3, in1=t3, op=ALU.mult)
+            nc.vector.scalar_tensor_tensor(out=p7v, in0=q, scalar=2.0, in1=t3, op0=ALU.subtract, op1=ALU.mult)
+            nc.vector.scalar_tensor_tensor(
+                out=tv[:, :, 5, :], in0=sq5v, scalar=1.25, in1=t1, op0=ALU.subtract, op1=ALU.mult
+            )
+            nc.gpsimd.tensor_tensor(out=tv[:, :, 7, :], in0=p7v, in1=t1, op=ALU.subtract)
+
+        def turn(u):
+            tt = tts[u % TT_BUFS]
+            g = work.tile([P, UNIT * K_ALL], BF16, name="grp", align_bytes=64)
+            cd = work.tile([P, UNIT * P], U32, name="cod", align_bytes=64)
+            sc = work.tile([P, UNIT * P], U8, name="scl", align_bytes=64)
+            grouped[u], codes[u], scales[u] = g, cd, sc
+            for t in range(UNIT):
+                ps = tps.tile([P, 4 * P], F32, name="tp", tag="tp")
+                for a in range(4):
+                    nc.tensor.transpose(
+                        out=ps[:, a * P : (a + 1) * P],
+                        in_=tt[:, (t * 4 + a) * P : (t * 4 + a + 1) * P],
+                        identity=ident[:],
+                    )
+                dst = g[:, t * K_ALL : (t + 1) * K_ALL].rearrange("p (n a) -> p n a", a=4)
+                src = ps[:].rearrange("p (a n) -> p n a", a=4)
+                if t in VEC_EVAC[u % 2]:
+                    nc.vector.tensor_scalar(
+                        out=dst, in0=src, scalar1=fac[:, 0:1], scalar2=add[:, 0:1], op0=ALU.mult, op1=ALU.add
+                    )
+                else:
+                    nc.scalar.activation(out=dst, in_=src, func=ACT.Identity, bias=add[:, 0:1], scale=fac[:, 0:1])
+                if t % 4 == 3:
+                    h = t // 4
+                    nc.vector.quantize_mx(
+                        out=cd[:, h * 512 : (h + 1) * 512].bitcast(FP8X4),
+                        scales=sc[:, h * 512 : (h + 1) * 512],
+                        in_=g[:, h * 2048 : (h + 1) * 2048],
+                    )
+
+        def multiply(u):
+            cd, sc = codes[u], scales[u]
+            ob = outp.tile([P, UNIT, N_OUT], F32, name="ob")
+            for pr in range(UNIT // 2):
+                po = ops.tile([P, 2, N_OUT], F32, name="po")
+                for e in range(2):
+                    t = pr * 2 + e
+                    nc.tensor.matmul_mx(
+                        out=po[:, e, :],
+                        lhsT=cd[:, t * P : (t + 1) * P].bitcast(FP8X4),
+                        lhsT_scale=sc[:, t * P : (t + 1) * P],
+                        rhs=w_codes[:].bitcast(FP8X4),
+                        rhs_scale=w_scales[:],
+                        start=True,
+                        stop=True,
+                    )
+                nc.vector.tensor_tensor(out=ob[:, pr * 2 : pr * 2 + 2, :], in0=po[:], in1=bias_f[:], op=ALU.add)
+            nc.sync.dma_start(out=out_rows[:, u * UNIT : (u + 1) * UNIT, :], in_=ob[:])
+
+        for step in range(N_UNITS + 2):
+            if step < N_UNITS:
+                gen(step)
+            if 0 <= step - 1 < N_UNITS:
+                turn(step - 1)
+            if 0 <= step - 2 < N_UNITS:
+                multiply(step - 2)

@@ -21,7 +21,7 @@ UNIT = 8
 N_UNITS = NB // UNIT
 X_CHUNKS = (1, 3, 4, 8)
 TT_BUFS = 3
-VEC_EVAC = ((3, 7), (7,))
+VEC_EVAC = ((7,), ())
 
 
 def tile_cfkanlayer_t_kernel(tc, x, cheby_coeffs, bias, out):
@@ -138,12 +138,12 @@ def tile_cfkanlayer_t_kernel(tc, x, cheby_coeffs, bias, out):
             nc.vector.scalar_tensor_tensor(out=t3, in0=s4, scalar=3.0, in1=t1, op0=ALU.subtract, op1=ALU.mult)
             nc.scalar.activation(out=q, in_=s4, func=ACT.Square, bias=shifts[:, 0:1])
             nc.scalar.activation(out=sq5v, in_=s4, func=ACT.Square, bias=shifts[:, 1:2])
-            nc.gpsimd.tensor_tensor(out=tv[:, :, 6, :], in0=t3, in1=t3, op=ALU.mult)
+            nc.vector.tensor_tensor(out=tv[:, :, 6, :], in0=t3, in1=t3, op=ALU.mult)
             nc.vector.scalar_tensor_tensor(out=p7v, in0=q, scalar=2.0, in1=t3, op0=ALU.subtract, op1=ALU.mult)
             nc.vector.scalar_tensor_tensor(
                 out=tv[:, :, 5, :], in0=sq5v, scalar=1.25, in1=t1, op0=ALU.subtract, op1=ALU.mult
             )
-            nc.gpsimd.tensor_tensor(out=tv[:, :, 7, :], in0=p7v, in1=t1, op=ALU.subtract)
+            nc.vector.tensor_tensor(out=tv[:, :, 7, :], in0=p7v, in1=t1, op=ALU.subtract)
 
         def turn(u):
             tt = tts[u % TT_BUFS]

@@ -17,34 +17,35 @@ K_ALL = D_IN * N_DEG
 FLOPS = 2 * N_ROWS * K_ALL * N_OUT
 
 NB = N_ROWS // P
-UNIT = 8
-N_UNITS = NB // UNIT
-X_CHUNKS = (1, 3, 4, 8)
-TT_BUFS = 3
-VEC_EVAC = ((7,), ())
+UNITS = [4, 4] + [8] * 14 + [4, 4]
+MAX_UNIT = max(UNITS)
+X_CHUNKS = (8, 24, 32, 64)
+TT_BUFS = 5
+W_PLANE = D_IN
+W_TURN = K_ALL + 40
+W_QUANT = 135
+W_BIAS = N_OUT
 
 
 def tile_cfkanlayer_t_kernel(tc, x, cheby_coeffs, bias, out):
     nc = tc.nc
+    assert sum(UNITS) == NB and sum(X_CHUNKS) == NB
     with ExitStack() as ctx:
         const = ctx.enter_context(tc.tile_pool(name="const", bufs=1))
         work = ctx.enter_context(tc.tile_pool(name="work", bufs=3))
         outp = ctx.enter_context(tc.tile_pool(name="outp", bufs=4))
-        tps = ctx.enter_context(tc.psum_pool(name="tps", bufs=5))
-        ops = ctx.enter_context(tc.psum_pool(name="ops", bufs=3))
+        tps = ctx.enter_context(tc.psum_pool(name="tps", bufs=4))
+        ops = ctx.enter_context(tc.psum_pool(name="ops", bufs=4))
 
         x_rows = x.rearrange("(p t) d -> p (t d)", t=NB)
-        x_tiles = []
-        unit_src = []
+        x_of_block = []
         first = 0
-        for ci, n_units in enumerate(X_CHUNKS):
-            width = n_units * UNIT * D_IN
-            xt = const.tile([P, width], BF16, name="x%d" % ci)
-            nc.sync.dma_start(out=xt[:], in_=x_rows[:, first * UNIT * D_IN : first * UNIT * D_IN + width])
-            x_tiles.append(xt)
-            for j in range(n_units):
-                unit_src.append((ci, j))
-            first += n_units
+        for ci, n_blocks in enumerate(X_CHUNKS):
+            xt = const.tile([P, n_blocks * D_IN], BF16, name="x%d" % ci)
+            nc.sync.dma_start(out=xt[:], in_=x_rows[:, first * D_IN : (first + n_blocks) * D_IN])
+            for j in range(n_blocks):
+                x_of_block.append((xt, j))
+            first += n_blocks
 
         w_raw = const.tile([P, 2, K_ALL], BF16, name="w_raw")
         nc.scalar.dma_start(out=w_raw[:], in_=cheby_coeffs.rearrange("(h p) d k -> p h (d k)", p=P))
@@ -58,6 +59,16 @@ def tile_cfkanlayer_t_kernel(tc, x, cheby_coeffs, bias, out):
         nc.vector.memset(shifts[:, 0:1], -2.0)
         nc.vector.memset(shifts[:, 1:2], -2.5)
         nc.vector.memset(shifts[:, 2:3], 1.0)
+
+        tts = []
+        for b in range(TT_BUFS):
+            tt = const.tile([P, MAX_UNIT * K_ALL], F32, name="tt%d" % b)
+            tts.append(tt)
+            nc.scalar.activation(
+                out=tt[:].rearrange("p (x k i) -> p x k i", k=N_DEG, i=4)[:, :, 0, :],
+                in_=shifts[:, 2:3].unsqueeze(2).to_broadcast([P, MAX_UNIT * D_IN // 4, 4]),
+                func=ACT.Identity,
+            )
 
         pat = const.tile([P, P], F32, name="pat")
         pat_v = pat[:].rearrange("p (c k i) -> p c k i", c=4, k=N_DEG, i=4)
@@ -75,10 +86,6 @@ def tile_cfkanlayer_t_kernel(tc, x, cheby_coeffs, bias, out):
         add = const.tile([P, 1], F32, name="add")
         nc.vector.tensor_copy(out=fac[:], in_=pat_ps[:, 0:1])
         nc.vector.tensor_copy(out=add[:], in_=pat_ps[:, 64:65])
-
-        bias_f = const.tile([P, 2, N_OUT], F32, name="bias_f")
-        nc.vector.tensor_copy(out=bias_f[:, 0, :], in_=bias_bf[:])
-        nc.vector.tensor_copy(out=bias_f[:, 1, :], in_=bias_bf[:])
 
         w_f = const.tile([P, 2 * K_ALL], F32, name="w_f")
         nc.vector.tensor_copy(
@@ -105,53 +112,69 @@ def tile_cfkanlayer_t_kernel(tc, x, cheby_coeffs, bias, out):
             scales=w_scales[:],
             in_=w_grp[:].rearrange("p o a -> p (o a)"),
         )
+        bias_f = const.tile([P, 2, N_OUT], F32, name="bias_f")
+        nc.vector.tensor_copy(out=bias_f[:, 0, :], in_=bias_bf[:])
+        nc.vector.tensor_copy(out=bias_f[:, 1, :], in_=bias_bf[:])
 
-        tts = []
-        for b in range(TT_BUFS):
-            tt = const.tile([P, UNIT * K_ALL], F32, name="tt%d" % b)
-            tts.append(tt)
-            nc.scalar.activation(
-                out=tt[:].rearrange("p (x k i) -> p x k i", k=N_DEG, i=4)[:, :, 0, :],
-                in_=shifts[:, 2:3].unsqueeze(2).to_broadcast([P, UNIT * D_IN // 4, 4]),
-                func=ACT.Identity,
-            )
-
-        grouped = {}
+        starts = [sum(UNITS[:u]) for u in range(len(UNITS))]
+        n_units = len(UNITS)
+        sq5s = {}
+        groups = {}
         codes = {}
         scales = {}
+        banks = {}
+        load = [0, 0]
         out_rows = out.rearrange("(p t) o -> p t o", t=NB)
 
-        def gen(u):
-            ci, j = unit_src[u]
-            xs = x_tiles[ci][:, j * UNIT * D_IN : (j + 1) * UNIT * D_IN].rearrange("p (x i) -> p x i", i=4)
-            tv = tts[u % TT_BUFS][:].rearrange("p (x k i) -> p x k i", k=N_DEG, i=4)
+        def planes(u):
+            return tts[u % TT_BUFS][:, 0 : UNITS[u] * K_ALL].rearrange("p (x k i) -> p x k i", k=N_DEG, i=4)
+
+        def gen_scalar(u):
+            n = UNITS[u]
+            xt, j = x_of_block[starts[u]]
+            xs = xt[:, j * D_IN : (j + n) * D_IN].rearrange("p (x i) -> p x i", i=4)
+            tv = planes(u)
+            sq5 = work.tile([P, MAX_UNIT * D_IN], F32, name="sq5")
+            sq5s[u] = sq5
+            nc.scalar.activation(out=tv[:, :, 1, :], in_=xs, func=ACT.Tanh)
+            nc.scalar.activation(out=tv[:, :, 2, :], in_=tv[:, :, 1, :], func=ACT.Square, scale=2.0)
+            nc.scalar.activation(out=tv[:, :, 4, :], in_=tv[:, :, 2, :], func=ACT.Square, bias=shifts[:, 0:1])
+            nc.scalar.activation(
+                out=sq5[:, 0 : n * D_IN].rearrange("p (x i) -> p x i", i=4),
+                in_=tv[:, :, 2, :],
+                func=ACT.Square,
+                bias=shifts[:, 1:2],
+            )
+
+        def gen_vector(u):
+            n = UNITS[u]
+            tv = planes(u)
             t1 = tv[:, :, 1, :]
-            s4 = tv[:, :, 2, :]
             t3 = tv[:, :, 3, :]
-            q = tv[:, :, 4, :]
-            sq5 = work.tile([P, UNIT * D_IN], F32, name="sq5")
-            p7 = work.tile([P, UNIT * D_IN], F32, name="p7")
-            sq5v = sq5[:].rearrange("p (x i) -> p x i", i=4)
-            p7v = p7[:].rearrange("p (x i) -> p x i", i=4)
-            nc.scalar.activation(out=t1, in_=xs, func=ACT.Tanh)
-            nc.scalar.activation(out=s4, in_=t1, func=ACT.Square, scale=2.0)
-            nc.vector.scalar_tensor_tensor(out=t3, in0=s4, scalar=3.0, in1=t1, op0=ALU.subtract, op1=ALU.mult)
-            nc.scalar.activation(out=q, in_=s4, func=ACT.Square, bias=shifts[:, 0:1])
-            nc.scalar.activation(out=sq5v, in_=s4, func=ACT.Square, bias=shifts[:, 1:2])
-            nc.vector.tensor_tensor(out=tv[:, :, 6, :], in0=t3, in1=t3, op=ALU.mult)
-            nc.vector.scalar_tensor_tensor(out=p7v, in0=q, scalar=2.0, in1=t3, op0=ALU.subtract, op1=ALU.mult)
+            sq5v = sq5s[u][:, 0 : n * D_IN].rearrange("p (x i) -> p x i", i=4)
+            p7 = work.tile([P, MAX_UNIT * D_IN], F32, name="p7")
+            p7v = p7[:, 0 : n * D_IN].rearrange("p (x i) -> p x i", i=4)
             nc.vector.scalar_tensor_tensor(
                 out=tv[:, :, 5, :], in0=sq5v, scalar=1.25, in1=t1, op0=ALU.subtract, op1=ALU.mult
             )
-            nc.vector.tensor_tensor(out=tv[:, :, 7, :], in0=p7v, in1=t1, op=ALU.subtract)
+            nc.vector.scalar_tensor_tensor(
+                out=t3, in0=tv[:, :, 2, :], scalar=3.0, in1=t1, op0=ALU.subtract, op1=ALU.mult
+            )
+            nc.vector.scalar_tensor_tensor(
+                out=p7v, in0=tv[:, :, 4, :], scalar=2.0, in1=t3, op0=ALU.subtract, op1=ALU.mult
+            )
+            eng = nc.gpsimd
+            eng.tensor_tensor(out=tv[:, :, 6, :], in0=t3, in1=t3, op=ALU.mult)
+            eng.tensor_tensor(out=tv[:, :, 7, :], in0=p7v, in1=t1, op=ALU.subtract)
 
-        def turn(u):
+        def turn(u, part):
+            n = UNITS[u]
             tt = tts[u % TT_BUFS]
-            g = work.tile([P, UNIT * K_ALL], BF16, name="grp", align_bytes=64)
-            cd = work.tile([P, UNIT * P], U32, name="cod", align_bytes=64)
-            sc = work.tile([P, UNIT * P], U8, name="scl", align_bytes=64)
-            grouped[u], codes[u], scales[u] = g, cd, sc
-            for t in range(UNIT):
+            if part == 0:
+                grp = work.tile([P, MAX_UNIT * K_ALL], BF16, name="grp", align_bytes=64)
+                groups[u] = grp
+            g = groups[u]
+            for t in range(part * n // 2, (part + 1) * n // 2):
                 ps = tps.tile([P, 4 * P], F32, name="tp", tag="tp")
                 for a in range(4):
                     nc.tensor.transpose(
@@ -161,25 +184,30 @@ def tile_cfkanlayer_t_kernel(tc, x, cheby_coeffs, bias, out):
                     )
                 dst = g[:, t * K_ALL : (t + 1) * K_ALL].rearrange("p (n a) -> p n a", a=4)
                 src = ps[:].rearrange("p (a n) -> p n a", a=4)
-                if t in VEC_EVAC[u % 2]:
+                if load[1] < load[0]:
                     nc.vector.tensor_scalar(
                         out=dst, in0=src, scalar1=fac[:, 0:1], scalar2=add[:, 0:1], op0=ALU.mult, op1=ALU.add
                     )
+                    load[1] += W_TURN
                 else:
                     nc.scalar.activation(out=dst, in_=src, func=ACT.Identity, bias=add[:, 0:1], scale=fac[:, 0:1])
-                if t % 4 == 3:
-                    h = t // 4
-                    nc.vector.quantize_mx(
-                        out=cd[:, h * 512 : (h + 1) * 512].bitcast(FP8X4),
-                        scales=sc[:, h * 512 : (h + 1) * 512],
-                        in_=g[:, h * 2048 : (h + 1) * 2048],
-                    )
+                    load[0] += W_TURN
+
+        def quantise(u):
+            n = UNITS[u]
+            cd = work.tile([P, MAX_UNIT * P], U32, name="cod", align_bytes=64)
+            sc = work.tile([P, MAX_UNIT * P], U8, name="scl", align_bytes=64)
+            codes[u], scales[u] = cd, sc
+            nc.vector.quantize_mx(
+                out=cd[:, 0 : n * P].bitcast(FP8X4), scales=sc[:, 0 : n * P], in_=groups[u][:, 0 : n * K_ALL]
+            )
 
         def multiply(u):
             cd, sc = codes[u], scales[u]
-            ob = outp.tile([P, UNIT, N_OUT], F32, name="ob")
-            for pr in range(UNIT // 2):
+            banks[u] = []
+            for pr in range(UNITS[u] // 2):
                 po = ops.tile([P, 2, N_OUT], F32, name="po")
+                banks[u].append(po)
                 for e in range(2):
                     t = pr * 2 + e
                     nc.tensor.matmul_mx(
@@ -191,13 +219,32 @@ def tile_cfkanlayer_t_kernel(tc, x, cheby_coeffs, bias, out):
                         start=True,
                         stop=True,
                     )
-                nc.vector.tensor_tensor(out=ob[:, pr * 2 : pr * 2 + 2, :], in0=po[:], in1=bias_f[:], op=ALU.add)
-            nc.sync.dma_start(out=out_rows[:, u * UNIT : (u + 1) * UNIT, :], in_=ob[:])
 
-        for step in range(N_UNITS + 2):
-            if step < N_UNITS:
-                gen(step)
-            if 0 <= step - 1 < N_UNITS:
-                turn(step - 1)
-            if 0 <= step - 2 < N_UNITS:
-                multiply(step - 2)
+        def finish(u):
+            n = UNITS[u]
+            ob = outp.tile([P, MAX_UNIT, N_OUT], F32, name="ob")
+            for pr, po in enumerate(banks[u]):
+                nc.vector.tensor_tensor(out=ob[:, pr * 2 : pr * 2 + 2, :], in0=po[:], in1=bias_f[:], op=ALU.add)
+            nc.sync.dma_start(out=out_rows[:, starts[u] : starts[u] + n, :], in_=ob[:, 0:n, :])
+
+        with tc.manual_schedule():
+            for s in range(n_units + 4):
+                if s < n_units:
+                    load[0] += 4 * UNITS[s] * W_PLANE
+                if 0 <= s - 1 < n_units:
+                    load[1] += 3 * UNITS[s - 1] * W_PLANE
+                if 0 <= s - 4 < n_units:
+                    load[1] += UNITS[s - 4] * (W_QUANT + W_BIAS)
+                if 0 <= s - 3 < n_units:
+                    turn(s - 3, 0)
+                if 0 <= s - 4 < n_units:
+                    quantise(s - 4)
+                    multiply(s - 4)
+                if s < n_units:
+                    gen_scalar(s)
+                if 0 <= s - 1 < n_units:
+                    gen_vector(s - 1)
+                if 0 <= s - 4 < n_units:
+                    finish(s - 4)
+                if 0 <= s - 3 < n_units:
+                    turn(s - 3, 1)

@@ -17,14 +17,14 @@ K_ALL = D_IN * N_DEG
 FLOPS = 2 * N_ROWS * K_ALL * N_OUT
 
 NB = N_ROWS // P
-UNITS = [4, 4] + [8] * 14 + [4, 4]
+UNITS = [8] * 16
 MAX_UNIT = max(UNITS)
 X_CHUNKS = (8, 24, 32, 64)
-TT_BUFS = 5
-W_PLANE = D_IN
-W_TURN = K_ALL + 40
-W_QUANT = 135
-W_BIAS = N_OUT
+TT_BUFS = 3
+VEC_EVAC = (15,)
+VEC_MOD = 16
+G_SPLIT = 1
+DUMMIES = (1, 2)
 
 
 def tile_cfkanlayer_t_kernel(tc, x, cheby_coeffs, bias, out):
@@ -35,7 +35,8 @@ def tile_cfkanlayer_t_kernel(tc, x, cheby_coeffs, bias, out):
         work = ctx.enter_context(tc.tile_pool(name="work", bufs=3))
         outp = ctx.enter_context(tc.tile_pool(name="outp", bufs=4))
         tps = ctx.enter_context(tc.psum_pool(name="tps", bufs=4))
-        ops = ctx.enter_context(tc.psum_pool(name="ops", bufs=4))
+        ops = ctx.enter_context(tc.psum_pool(name="ops", bufs=3))
+        scr = ctx.enter_context(tc.psum_pool(name="scr", bufs=1))
 
         x_rows = x.rearrange("(p t) d -> p (t d)", t=NB)
         x_of_block = []
@@ -105,76 +106,65 @@ def tile_cfkanlayer_t_kernel(tc, x, cheby_coeffs, bias, out):
                 out=w_grp[:, h * P : (h + 1) * P, :],
                 in_=w_ps[:].rearrange("p (a o) -> p o a", a=4),
             )
-        w_codes = const.tile([P, N_OUT], U32, name="w_codes", align_bytes=64)
-        w_scales = const.tile([P, N_OUT], U8, name="w_scales", align_bytes=64)
-        nc.vector.quantize_mx(
-            out=w_codes[:].bitcast(FP8X4),
-            scales=w_scales[:],
-            in_=w_grp[:].rearrange("p o a -> p (o a)"),
-        )
+        w_codes = const.tile([P, 2 * N_OUT], U32, name="w_codes", align_bytes=64)
+        w_scales = const.tile([P, 2 * N_OUT], U8, name="w_scales", align_bytes=64)
+        for h in range(2):
+            nc.vector.quantize_mx(
+                out=w_codes[:, h * N_OUT : (h + 1) * N_OUT].bitcast(FP8X4),
+                scales=w_scales[:, h * N_OUT : (h + 1) * N_OUT],
+                in_=w_grp[:].rearrange("p o a -> p (o a)"),
+            )
+        idle_bank = scr.tile([P, 2 * N_OUT], F32, name="idle_bank")
         bias_f = const.tile([P, 2, N_OUT], F32, name="bias_f")
         nc.vector.tensor_copy(out=bias_f[:, 0, :], in_=bias_bf[:])
         nc.vector.tensor_copy(out=bias_f[:, 1, :], in_=bias_bf[:])
 
         starts = [sum(UNITS[:u]) for u in range(len(UNITS))]
-        n_units = len(UNITS)
-        sq5s = {}
-        groups = {}
         codes = {}
         scales = {}
-        banks = {}
-        load = [0, 0]
         out_rows = out.rearrange("(p t) o -> p t o", t=NB)
 
-        def planes(u):
-            return tts[u % TT_BUFS][:, 0 : UNITS[u] * K_ALL].rearrange("p (x k i) -> p x k i", k=N_DEG, i=4)
-
-        def gen_scalar(u):
+        def gen(u):
             n = UNITS[u]
             xt, j = x_of_block[starts[u]]
+            assert x_of_block[starts[u] + n - 1][0] is xt
             xs = xt[:, j * D_IN : (j + n) * D_IN].rearrange("p (x i) -> p x i", i=4)
-            tv = planes(u)
-            sq5 = work.tile([P, MAX_UNIT * D_IN], F32, name="sq5")
-            sq5s[u] = sq5
-            nc.scalar.activation(out=tv[:, :, 1, :], in_=xs, func=ACT.Tanh)
-            nc.scalar.activation(out=tv[:, :, 2, :], in_=tv[:, :, 1, :], func=ACT.Square, scale=2.0)
-            nc.scalar.activation(out=tv[:, :, 4, :], in_=tv[:, :, 2, :], func=ACT.Square, bias=shifts[:, 0:1])
-            nc.scalar.activation(
-                out=sq5[:, 0 : n * D_IN].rearrange("p (x i) -> p x i", i=4),
-                in_=tv[:, :, 2, :],
-                func=ACT.Square,
-                bias=shifts[:, 1:2],
-            )
-
-        def gen_vector(u):
-            n = UNITS[u]
-            tv = planes(u)
+            tv = tts[u % TT_BUFS][:, 0 : n * K_ALL].rearrange("p (x k i) -> p x k i", k=N_DEG, i=4)
             t1 = tv[:, :, 1, :]
+            s4 = tv[:, :, 2, :]
             t3 = tv[:, :, 3, :]
-            sq5v = sq5s[u][:, 0 : n * D_IN].rearrange("p (x i) -> p x i", i=4)
+            q = tv[:, :, 4, :]
+            sq5 = work.tile([P, MAX_UNIT * D_IN], F32, name="sq5")
             p7 = work.tile([P, MAX_UNIT * D_IN], F32, name="p7")
+            sq5v = sq5[:, 0 : n * D_IN].rearrange("p (x i) -> p x i", i=4)
             p7v = p7[:, 0 : n * D_IN].rearrange("p (x i) -> p x i", i=4)
+            nc.scalar.activation(out=t1, in_=xs, func=ACT.Tanh)
+            nc.scalar.activation(out=s4, in_=t1, func=ACT.Square, scale=2.0)
+            nc.vector.scalar_tensor_tensor(out=t3, in0=s4, scalar=3.0, in1=t1, op0=ALU.subtract, op1=ALU.mult)
+            nc.scalar.activation(out=q, in_=s4, func=ACT.Square, bias=shifts[:, 0:1])
+            nc.scalar.activation(out=sq5v, in_=s4, func=ACT.Square, bias=shifts[:, 1:2])
+            nc.vector.scalar_tensor_tensor(out=p7v, in0=q, scalar=2.0, in1=t3, op0=ALU.subtract, op1=ALU.mult)
             nc.vector.scalar_tensor_tensor(
                 out=tv[:, :, 5, :], in0=sq5v, scalar=1.25, in1=t1, op0=ALU.subtract, op1=ALU.mult
             )
-            nc.vector.scalar_tensor_tensor(
-                out=t3, in0=tv[:, :, 2, :], scalar=3.0, in1=t1, op0=ALU.subtract, op1=ALU.mult
-            )
-            nc.vector.scalar_tensor_tensor(
-                out=p7v, in0=tv[:, :, 4, :], scalar=2.0, in1=t3, op0=ALU.subtract, op1=ALU.mult
-            )
-            eng = nc.gpsimd
-            eng.tensor_tensor(out=tv[:, :, 6, :], in0=t3, in1=t3, op=ALU.mult)
-            eng.tensor_tensor(out=tv[:, :, 7, :], in0=p7v, in1=t1, op=ALU.subtract)
+            eng = nc.vector
+            nx = n * D_IN // 4
+            for piece in range(G_SPLIT):
+                sl = slice(piece * nx // G_SPLIT, (piece + 1) * nx // G_SPLIT)
+                eng.tensor_tensor(out=tv[:, sl, 6, :], in0=t3[:, sl, :], in1=t3[:, sl, :], op=ALU.mult)
+            for piece in range(G_SPLIT):
+                sl = slice(piece * nx // G_SPLIT, (piece + 1) * nx // G_SPLIT)
+                eng.tensor_tensor(out=tv[:, sl, 7, :], in0=p7v[:, sl, :], in1=t1[:, sl, :], op=ALU.subtract)
 
-        def turn(u, part):
+        def turn(u):
             n = UNITS[u]
             tt = tts[u % TT_BUFS]
-            if part == 0:
-                grp = work.tile([P, MAX_UNIT * K_ALL], BF16, name="grp", align_bytes=64)
-                groups[u] = grp
-            g = groups[u]
-            for t in range(part * n // 2, (part + 1) * n // 2):
+            g = work.tile([P, MAX_UNIT * K_ALL], BF16, name="grp", align_bytes=64)
+            cd = work.tile([P, MAX_UNIT * P], U32, name="cod", align_bytes=64)
+            sc = work.tile([P, MAX_UNIT * P], U8, name="scl", align_bytes=64)
+            codes[u], scales[u] = cd, sc
+            qn = 2
+            for t in range(n):
                 ps = tps.tile([P, 4 * P], F32, name="tp", tag="tp")
                 for a in range(4):
                     nc.tensor.transpose(
@@ -184,67 +174,55 @@ def tile_cfkanlayer_t_kernel(tc, x, cheby_coeffs, bias, out):
                     )
                 dst = g[:, t * K_ALL : (t + 1) * K_ALL].rearrange("p (n a) -> p n a", a=4)
                 src = ps[:].rearrange("p (a n) -> p n a", a=4)
-                if load[1] < load[0]:
+                if (starts[u] + t) % VEC_MOD in VEC_EVAC:
                     nc.vector.tensor_scalar(
                         out=dst, in0=src, scalar1=fac[:, 0:1], scalar2=add[:, 0:1], op0=ALU.mult, op1=ALU.add
                     )
-                    load[1] += W_TURN
                 else:
                     nc.scalar.activation(out=dst, in_=src, func=ACT.Identity, bias=add[:, 0:1], scale=fac[:, 0:1])
-                    load[0] += W_TURN
-
-        def quantise(u):
-            n = UNITS[u]
-            cd = work.tile([P, MAX_UNIT * P], U32, name="cod", align_bytes=64)
-            sc = work.tile([P, MAX_UNIT * P], U8, name="scl", align_bytes=64)
-            codes[u], scales[u] = cd, sc
-            nc.vector.quantize_mx(
-                out=cd[:, 0 : n * P].bitcast(FP8X4), scales=sc[:, 0 : n * P], in_=groups[u][:, 0 : n * K_ALL]
-            )
+                if t % qn == qn - 1:
+                    h = t // qn
+                    nc.vector.quantize_mx(
+                        out=cd[:, h * qn * P : (h + 1) * qn * P].bitcast(FP8X4),
+                        scales=sc[:, h * qn * P : (h + 1) * qn * P],
+                        in_=g[:, h * qn * K_ALL : (h + 1) * qn * K_ALL],
+                    )
 
         def multiply(u):
+            n = UNITS[u]
             cd, sc = codes[u], scales[u]
-            banks[u] = []
-            for pr in range(UNITS[u] // 2):
+            ob = outp.tile([P, MAX_UNIT, N_OUT], F32, name="ob")
+            for pr in range(n // 2):
                 po = ops.tile([P, 2, N_OUT], F32, name="po")
-                banks[u].append(po)
                 for e in range(2):
                     t = pr * 2 + e
                     nc.tensor.matmul_mx(
                         out=po[:, e, :],
                         lhsT=cd[:, t * P : (t + 1) * P].bitcast(FP8X4),
                         lhsT_scale=sc[:, t * P : (t + 1) * P],
+                        rhs=w_codes[:, 0:N_OUT].bitcast(FP8X4),
+                        rhs_scale=w_scales[:, 0:N_OUT],
+                        start=True,
+                        stop=True,
+                    )
+                for extra in range(DUMMIES[pr % 2]):
+                    nc.tensor.matmul_mx(
+                        out=idle_bank[:],
+                        lhsT=cd[:, pr * 2 * P : (pr * 2 + 1) * P].bitcast(FP8X4),
+                        lhsT_scale=sc[:, pr * 2 * P : (pr * 2 + 1) * P],
                         rhs=w_codes[:].bitcast(FP8X4),
                         rhs_scale=w_scales[:],
                         start=True,
                         stop=True,
                     )
-
-        def finish(u):
-            n = UNITS[u]
-            ob = outp.tile([P, MAX_UNIT, N_OUT], F32, name="ob")
-            for pr, po in enumerate(banks[u]):
                 nc.vector.tensor_tensor(out=ob[:, pr * 2 : pr * 2 + 2, :], in0=po[:], in1=bias_f[:], op=ALU.add)
             nc.sync.dma_start(out=out_rows[:, starts[u] : starts[u] + n, :], in_=ob[:, 0:n, :])
 
-        with tc.manual_schedule():
-            for s in range(n_units + 4):
-                if s < n_units:
-                    load[0] += 4 * UNITS[s] * W_PLANE
-                if 0 <= s - 1 < n_units:
-                    load[1] += 3 * UNITS[s - 1] * W_PLANE
-                if 0 <= s - 4 < n_units:
-                    load[1] += UNITS[s - 4] * (W_QUANT + W_BIAS)
-                if 0 <= s - 3 < n_units:
-                    turn(s - 3, 0)
-                if 0 <= s - 4 < n_units:
-                    quantise(s - 4)
-                    multiply(s - 4)
-                if s < n_units:
-                    gen_scalar(s)
-                if 0 <= s - 1 < n_units:
-                    gen_vector(s - 1)
-                if 0 <= s - 4 < n_units:
-                    finish(s - 4)
-                if 0 <= s - 3 < n_units:
-                    turn(s - 3, 1)
+        n_units = len(UNITS)
+        for step in range(n_units + 2):
+            if step < n_units:
+                gen(step)
+            if 0 <= step - 1 < n_units:
+                turn(step - 1)
+            if 0 <= step - 2 < n_units:
+                multiply(step - 2)

@@ -20,11 +20,9 @@ NB = N_ROWS // P
 UNITS = [8] * 16
 MAX_UNIT = max(UNITS)
 X_CHUNKS = (8, 24, 32, 64)
-TT_BUFS = 3
-VEC_EVAC = (15,)
-VEC_MOD = 16
+TT_BUFS = 4
+VEC_EVAC = (15, 31, 47, 63, 79, 95, 111, 119)
 G_SPLIT = 1
-DUMMIES = (1, 2)
 
 
 def tile_cfkanlayer_t_kernel(tc, x, cheby_coeffs, bias, out):
@@ -32,11 +30,10 @@ def tile_cfkanlayer_t_kernel(tc, x, cheby_coeffs, bias, out):
     assert sum(UNITS) == NB and sum(X_CHUNKS) == NB
     with ExitStack() as ctx:
         const = ctx.enter_context(tc.tile_pool(name="const", bufs=1))
-        work = ctx.enter_context(tc.tile_pool(name="work", bufs=3))
+        work = ctx.enter_context(tc.tile_pool(name="work", bufs=4))
         outp = ctx.enter_context(tc.tile_pool(name="outp", bufs=4))
-        tps = ctx.enter_context(tc.psum_pool(name="tps", bufs=4))
+        tps = ctx.enter_context(tc.psum_pool(name="tps", bufs=5))
         ops = ctx.enter_context(tc.psum_pool(name="ops", bufs=3))
-        scr = ctx.enter_context(tc.psum_pool(name="scr", bufs=1))
 
         x_rows = x.rearrange("(p t) d -> p (t d)", t=NB)
         x_of_block = []
@@ -106,15 +103,13 @@ def tile_cfkanlayer_t_kernel(tc, x, cheby_coeffs, bias, out):
                 out=w_grp[:, h * P : (h + 1) * P, :],
                 in_=w_ps[:].rearrange("p (a o) -> p o a", a=4),
             )
-        w_codes = const.tile([P, 2 * N_OUT], U32, name="w_codes", align_bytes=64)
-        w_scales = const.tile([P, 2 * N_OUT], U8, name="w_scales", align_bytes=64)
-        for h in range(2):
-            nc.vector.quantize_mx(
-                out=w_codes[:, h * N_OUT : (h + 1) * N_OUT].bitcast(FP8X4),
-                scales=w_scales[:, h * N_OUT : (h + 1) * N_OUT],
-                in_=w_grp[:].rearrange("p o a -> p (o a)"),
-            )
-        idle_bank = scr.tile([P, 2 * N_OUT], F32, name="idle_bank")
+        w_codes = const.tile([P, N_OUT], U32, name="w_codes", align_bytes=64)
+        w_scales = const.tile([P, N_OUT], U8, name="w_scales", align_bytes=64)
+        nc.vector.quantize_mx(
+            out=w_codes[:].bitcast(FP8X4),
+            scales=w_scales[:],
+            in_=w_grp[:].rearrange("p o a -> p (o a)"),
+        )
         bias_f = const.tile([P, 2, N_OUT], F32, name="bias_f")
         nc.vector.tensor_copy(out=bias_f[:, 0, :], in_=bias_bf[:])
         nc.vector.tensor_copy(out=bias_f[:, 1, :], in_=bias_bf[:])
@@ -163,7 +158,7 @@ def tile_cfkanlayer_t_kernel(tc, x, cheby_coeffs, bias, out):
             cd = work.tile([P, MAX_UNIT * P], U32, name="cod", align_bytes=64)
             sc = work.tile([P, MAX_UNIT * P], U8, name="scl", align_bytes=64)
             codes[u], scales[u] = cd, sc
-            qn = 2
+            qn = min(n, 4)
             for t in range(n):
                 ps = tps.tile([P, 4 * P], F32, name="tp", tag="tp")
                 for a in range(4):
@@ -174,7 +169,7 @@ def tile_cfkanlayer_t_kernel(tc, x, cheby_coeffs, bias, out):
                     )
                 dst = g[:, t * K_ALL : (t + 1) * K_ALL].rearrange("p (n a) -> p n a", a=4)
                 src = ps[:].rearrange("p (a n) -> p n a", a=4)
-                if (starts[u] + t) % VEC_MOD in VEC_EVAC:
+                if starts[u] + t in VEC_EVAC:
                     nc.vector.tensor_scalar(
                         out=dst, in0=src, scalar1=fac[:, 0:1], scalar2=add[:, 0:1], op0=ALU.mult, op1=ALU.add
                     )
@@ -200,16 +195,6 @@ def tile_cfkanlayer_t_kernel(tc, x, cheby_coeffs, bias, out):
                         out=po[:, e, :],
                         lhsT=cd[:, t * P : (t + 1) * P].bitcast(FP8X4),
                         lhsT_scale=sc[:, t * P : (t + 1) * P],
-                        rhs=w_codes[:, 0:N_OUT].bitcast(FP8X4),
-                        rhs_scale=w_scales[:, 0:N_OUT],
-                        start=True,
-                        stop=True,
-                    )
-                for extra in range(DUMMIES[pr % 2]):
-                    nc.tensor.matmul_mx(
-                        out=idle_bank[:],
-                        lhsT=cd[:, pr * 2 * P : (pr * 2 + 1) * P].bitcast(FP8X4),
-                        lhsT_scale=sc[:, pr * 2 * P : (pr * 2 + 1) * P],
                         rhs=w_codes[:].bitcast(FP8X4),
                         rhs_scale=w_scales[:],
                         start=True,
@@ -219,10 +204,10 @@ def tile_cfkanlayer_t_kernel(tc, x, cheby_coeffs, bias, out):
             nc.sync.dma_start(out=out_rows[:, starts[u] : starts[u] + n, :], in_=ob[:, 0:n, :])
 
         n_units = len(UNITS)
-        for step in range(n_units + 2):
+        for step in range(n_units + 3):
             if step < n_units:
                 gen(step)
-            if 0 <= step - 1 < n_units:
-                turn(step - 1)
             if 0 <= step - 2 < n_units:
-                multiply(step - 2)
+                turn(step - 2)
+            if 0 <= step - 3 < n_units:
+                multiply(step - 3)

@@ -21,7 +21,7 @@ UNITS = [8] * 16
 MAX_UNIT = max(UNITS)
 X_CHUNKS = (8, 24, 32, 64)
 TT_BUFS = 4
-VEC_EVAC = (15, 31, 47, 63, 79, 95, 111, 119)
+VEC_EVAC = (7, 15, 23, 31, 39, 47, 55, 63, 71, 79, 87, 95, 103, 111, 119, 123)
 G_SPLIT = 1
 
 

@@ -21,7 +21,7 @@ UNITS = [8] * 16
 MAX_UNIT = max(UNITS)
 X_CHUNKS = (8, 24, 32, 64)
 TT_BUFS = 4
-VEC_EVAC = (7, 15, 23, 31, 39, 47, 55, 63, 71, 79, 87, 95, 103, 111, 119, 123)
+VEC_EVAC = ()
 G_SPLIT = 1
 
 

@@ -21,7 +21,7 @@ UNITS = [8] * 16
 MAX_UNIT = max(UNITS)
 X_CHUNKS = (8, 24, 32, 64)
 TT_BUFS = 4
-VEC_EVAC = ()
+VEC_EVAC = (31, 63, 95, 119)
 G_SPLIT = 1
 
 
@@ -201,7 +201,12 @@ def tile_cfkanlayer_t_kernel(tc, x, cheby_coeffs, bias, out):
                         stop=True,
                     )
                 nc.vector.tensor_tensor(out=ob[:, pr * 2 : pr * 2 + 2, :], in0=po[:], in1=bias_f[:], op=ALU.add)
-            nc.sync.dma_start(out=out_rows[:, starts[u] : starts[u] + n, :], in_=ob[:, 0:n, :])
+                if u == len(UNITS) - 1:
+                    nc.sync.dma_start(
+                        out=out_rows[:, starts[u] + pr * 2 : starts[u] + pr * 2 + 2, :], in_=ob[:, pr * 2 : pr * 2 + 2, :]
+                    )
+            if u < len(UNITS) - 1:
+                nc.sync.dma_start(out=out_rows[:, starts[u] : starts[u] + n, :], in_=ob[:, 0:n, :])
 
         n_units = len(UNITS)
         for step in range(n_units + 3):

@@ -17,23 +17,23 @@ K_ALL = D_IN * N_DEG
 FLOPS = 2 * N_ROWS * K_ALL * N_OUT
 
 NB = N_ROWS // P
-UNITS = [8] * 16
-MAX_UNIT = max(UNITS)
+TB = 8
+CH = P * 4
 X_CHUNKS = (8, 24, 32, 64)
-TT_BUFS = 4
-VEC_EVAC = (31, 63, 95, 119)
-G_SPLIT = 1
+L2_BUFS = 5
+LAG = 3
 
 
 def tile_cfkanlayer_t_kernel(tc, x, cheby_coeffs, bias, out):
     nc = tc.nc
-    assert sum(UNITS) == NB and sum(X_CHUNKS) == NB
+    assert sum(X_CHUNKS) == NB
     with ExitStack() as ctx:
         const = ctx.enter_context(tc.tile_pool(name="const", bufs=1))
-        work = ctx.enter_context(tc.tile_pool(name="work", bufs=4))
+        work = ctx.enter_context(tc.tile_pool(name="work", bufs=3))
+        cpool = ctx.enter_context(tc.tile_pool(name="cpool", bufs=4))
         outp = ctx.enter_context(tc.tile_pool(name="outp", bufs=4))
-        tps = ctx.enter_context(tc.psum_pool(name="tps", bufs=5))
-        ops = ctx.enter_context(tc.psum_pool(name="ops", bufs=3))
+        tps = ctx.enter_context(tc.psum_pool(name="tps", bufs=4))
+        ops = ctx.enter_context(tc.psum_pool(name="ops", bufs=4))
 
         x_rows = x.rearrange("(p t) d -> p (t d)", t=NB)
         x_of_block = []
@@ -44,7 +44,6 @@ def tile_cfkanlayer_t_kernel(tc, x, cheby_coeffs, bias, out):
             for j in range(n_blocks):
                 x_of_block.append((xt, j))
             first += n_blocks
-
         w_raw = const.tile([P, 2, K_ALL], BF16, name="w_raw")
         nc.scalar.dma_start(out=w_raw[:], in_=cheby_coeffs.rearrange("(h p) d k -> p h (d k)", p=P))
         bias_bf = const.tile([P, N_OUT], BF16, name="bias_bf")
@@ -52,56 +51,38 @@ def tile_cfkanlayer_t_kernel(tc, x, cheby_coeffs, bias, out):
 
         ident = const.tile([P, P], F32, name="ident")
         make_identity(nc, ident[:])
-
+        ident_bf = const.tile([P, P], BF16, name="ident_bf")
+        nc.vector.tensor_copy(out=ident_bf[:], in_=ident[:])
         shifts = const.tile([P, 3], F32, name="shifts")
         nc.vector.memset(shifts[:, 0:1], -2.0)
         nc.vector.memset(shifts[:, 1:2], -2.5)
-        nc.vector.memset(shifts[:, 2:3], 1.0)
+        nc.vector.memset(shifts[:, 2:3], -1.0)
+        ones = const.tile([P, CH], BF16, name="ones")
+        nc.vector.memset(ones[:], 1.0)
+        l2s = []
+        for b in range(L2_BUFS):
+            l2 = const.tile([P, TB * CH], BF16, name="l2_%d" % b, align_bytes=64)
+            nc.sync.dma_start(out=l2[0:P:8, :], in_=ones[:])
+            l2s.append(l2)
 
-        tts = []
-        for b in range(TT_BUFS):
-            tt = const.tile([P, MAX_UNIT * K_ALL], F32, name="tt%d" % b)
-            tts.append(tt)
-            nc.scalar.activation(
-                out=tt[:].rearrange("p (x k i) -> p x k i", k=N_DEG, i=4)[:, :, 0, :],
-                in_=shifts[:, 2:3].unsqueeze(2).to_broadcast([P, MAX_UNIT * D_IN // 4, 4]),
-                func=ACT.Identity,
+        w_re = const.tile([P, 2, K_ALL], BF16, name="w_re")
+        for h in range(2):
+            nc.vector.tensor_copy(
+                out=w_re[:, h, :].rearrange("p (i g k) -> p i g k", i=4, k=N_DEG),
+                in_=w_raw[:, h, :].rearrange("p (g i k) -> p i g k", i=4, k=N_DEG),
             )
-
-        pat = const.tile([P, P], F32, name="pat")
-        pat_v = pat[:].rearrange("p (c k i) -> p c k i", c=4, k=N_DEG, i=4)
-        nc.vector.memset(pat[0:64, :], 1.0)
-        nc.vector.memset(pat_v[0:64, :, 2, :], 0.5)
-        nc.vector.memset(pat_v[0:64, :, 4, :], 0.5)
-        nc.vector.memset(pat_v[0:64, :, 6, :], 2.0)
-        nc.vector.memset(pat[64:128, :], 0.0)
-        nc.vector.memset(pat_v[64:128, :, 2, :], -1.0)
-        nc.vector.memset(pat_v[64:128, :, 4, :], -1.0)
-        nc.vector.memset(pat_v[64:128, :, 6, :], -1.0)
-        pat_ps = tps.tile([P, 4 * P], F32, name="pat_ps", tag="tp")
-        nc.tensor.transpose(out=pat_ps[:, 0:P], in_=pat[:], identity=ident[:])
-        fac = const.tile([P, 1], F32, name="fac")
-        add = const.tile([P, 1], F32, name="add")
-        nc.vector.tensor_copy(out=fac[:], in_=pat_ps[:, 0:1])
-        nc.vector.tensor_copy(out=add[:], in_=pat_ps[:, 64:65])
-
-        w_f = const.tile([P, 2 * K_ALL], F32, name="w_f")
-        nc.vector.tensor_copy(
-            out=w_f[:].rearrange("p (g k i) -> p g k i", k=N_DEG, i=4),
-            in_=w_raw[:].rearrange("p h (g i k) -> p (h g) k i", i=4, k=N_DEG),
-        )
         w_grp = const.tile([P, N_OUT, 4], BF16, name="w_grp", align_bytes=64)
         for h in range(2):
-            w_ps = tps.tile([P, 4 * P], F32, name="w_ps", tag="tp")
-            for a in range(4):
+            w_ps = tps.tile([P, 4 * P], BF16, name="w_ps", tag="tp")
+            for i in range(4):
                 nc.tensor.transpose(
-                    out=w_ps[:, a * P : (a + 1) * P],
-                    in_=w_f[:, (h * 4 + a) * P : (h * 4 + a + 1) * P],
-                    identity=ident[:],
+                    out=w_ps[:, i * P : (i + 1) * P],
+                    in_=w_re[:, h, i * P : (i + 1) * P],
+                    identity=ident_bf[:],
                 )
             nc.vector.tensor_copy(
                 out=w_grp[:, h * P : (h + 1) * P, :],
-                in_=w_ps[:].rearrange("p (a o) -> p o a", a=4),
+                in_=w_ps[:].rearrange("p (i o) -> p o i", i=4),
             )
         w_codes = const.tile([P, N_OUT], U32, name="w_codes", align_bytes=64)
         w_scales = const.tile([P, N_OUT], U8, name="w_scales", align_bytes=64)
@@ -114,105 +95,146 @@ def tile_cfkanlayer_t_kernel(tc, x, cheby_coeffs, bias, out):
         nc.vector.tensor_copy(out=bias_f[:, 0, :], in_=bias_bf[:])
         nc.vector.tensor_copy(out=bias_f[:, 1, :], in_=bias_bf[:])
 
-        starts = [sum(UNITS[:u]) for u in range(len(UNITS))]
-        codes = {}
-        scales = {}
         out_rows = out.rearrange("(p t) o -> p t o", t=NB)
 
-        def gen(u):
-            n = UNITS[u]
-            xt, j = x_of_block[starts[u]]
-            assert x_of_block[starts[u] + n - 1][0] is xt
-            xs = xt[:, j * D_IN : (j + n) * D_IN].rearrange("p (x i) -> p x i", i=4)
-            tv = tts[u % TT_BUFS][:, 0 : n * K_ALL].rearrange("p (x k i) -> p x k i", k=N_DEG, i=4)
-            t1 = tv[:, :, 1, :]
-            s4 = tv[:, :, 2, :]
-            t3 = tv[:, :, 3, :]
-            q = tv[:, :, 4, :]
-            sq5 = work.tile([P, MAX_UNIT * D_IN], F32, name="sq5")
-            p7 = work.tile([P, MAX_UNIT * D_IN], F32, name="p7")
-            sq5v = sq5[:, 0 : n * D_IN].rearrange("p (x i) -> p x i", i=4)
-            p7v = p7[:, 0 : n * D_IN].rearrange("p (x i) -> p x i", i=4)
-            nc.scalar.activation(out=t1, in_=xs, func=ACT.Tanh)
-            nc.scalar.activation(out=s4, in_=t1, func=ACT.Square, scale=2.0)
-            nc.vector.scalar_tensor_tensor(out=t3, in0=s4, scalar=3.0, in1=t1, op0=ALU.subtract, op1=ALU.mult)
-            nc.scalar.activation(out=q, in_=s4, func=ACT.Square, bias=shifts[:, 0:1])
-            nc.scalar.activation(out=sq5v, in_=s4, func=ACT.Square, bias=shifts[:, 1:2])
-            nc.vector.scalar_tensor_tensor(out=p7v, in0=q, scalar=2.0, in1=t3, op0=ALU.subtract, op1=ALU.mult)
-            nc.vector.scalar_tensor_tensor(
-                out=tv[:, :, 5, :], in0=sq5v, scalar=1.25, in1=t1, op0=ALU.subtract, op1=ALU.mult
-            )
-            eng = nc.vector
-            nx = n * D_IN // 4
-            for piece in range(G_SPLIT):
-                sl = slice(piece * nx // G_SPLIT, (piece + 1) * nx // G_SPLIT)
-                eng.tensor_tensor(out=tv[:, sl, 6, :], in0=t3[:, sl, :], in1=t3[:, sl, :], op=ALU.mult)
-            for piece in range(G_SPLIT):
-                sl = slice(piece * nx // G_SPLIT, (piece + 1) * nx // G_SPLIT)
-                eng.tensor_tensor(out=tv[:, sl, 7, :], in0=p7v[:, sl, :], in1=t1[:, sl, :], op=ALU.subtract)
+        live = {}
+        n_units = NB // TB
+
+        def by_row(tile):
+            return tile[:].rearrange("q (p i) -> q p i", i=4)
+
+        def send(u, k):
+            nc.sync.dma_start(out=l2s[u % L2_BUFS][k:P:8, :], in_=live[u][k][:])
 
         def turn(u):
-            n = UNITS[u]
-            tt = tts[u % TT_BUFS]
-            g = work.tile([P, MAX_UNIT * K_ALL], BF16, name="grp", align_bytes=64)
-            cd = work.tile([P, MAX_UNIT * P], U32, name="cod", align_bytes=64)
-            sc = work.tile([P, MAX_UNIT * P], U8, name="scl", align_bytes=64)
-            codes[u], scales[u] = cd, sc
-            qn = min(n, 4)
-            for t in range(n):
-                ps = tps.tile([P, 4 * P], F32, name="tp", tag="tp")
-                for a in range(4):
-                    nc.tensor.transpose(
-                        out=ps[:, a * P : (a + 1) * P],
-                        in_=tt[:, (t * 4 + a) * P : (t * 4 + a + 1) * P],
-                        identity=ident[:],
-                    )
-                dst = g[:, t * K_ALL : (t + 1) * K_ALL].rearrange("p (n a) -> p n a", a=4)
-                src = ps[:].rearrange("p (a n) -> p n a", a=4)
-                if starts[u] + t in VEC_EVAC:
-                    nc.vector.tensor_scalar(
-                        out=dst, in0=src, scalar1=fac[:, 0:1], scalar2=add[:, 0:1], op0=ALU.mult, op1=ALU.add
-                    )
-                else:
-                    nc.scalar.activation(out=dst, in_=src, func=ACT.Identity, bias=add[:, 0:1], scale=fac[:, 0:1])
-                if t % qn == qn - 1:
-                    h = t // qn
-                    nc.vector.quantize_mx(
-                        out=cd[:, h * qn * P : (h + 1) * qn * P].bitcast(FP8X4),
-                        scales=sc[:, h * qn * P : (h + 1) * qn * P],
-                        in_=g[:, h * qn * K_ALL : (h + 1) * qn * K_ALL],
-                    )
+            lv = {}
+            live[u] = lv
+            for k in range(1, N_DEG):
+                lv[k] = work.tile([P, CH], BF16, name="pl%d" % k)
+            tr = work.tile([P, CH], F32, name="tr")
+            xt, j = x_of_block[u * TB]
+            nc.scalar.activation(
+                out=tr[:].rearrange("p (i g t) -> p g t i", i=4, t=TB),
+                in_=xt[:, j * D_IN : (j + TB) * D_IN].rearrange("p (t g i) -> p g t i", t=TB, i=4),
+                func=ACT.Tanh,
+            )
+            ps = tps.tile([P, CH], F32, name="tp", tag="tp")
+            for i in range(4):
+                nc.tensor.transpose(out=ps[:, i * P : (i + 1) * P], in_=tr[:, i * P : (i + 1) * P], identity=ident[:])
+            lv["t"] = ps[:].rearrange("q (i p) -> q p i", i=4)
 
-        def multiply(u):
-            n = UNITS[u]
-            cd, sc = codes[u], scales[u]
-            ob = outp.tile([P, MAX_UNIT, N_OUT], F32, name="ob")
-            for pr in range(n // 2):
+        def squares(u):
+            lv = live[u]
+            lv["s4"] = work.tile([P, CH], F32, name="s4")
+            lv["q"] = work.tile([P, CH], F32, name="q")
+            lv["sq5"] = work.tile([P, CH], F32, name="sq5")
+            nc.scalar.activation(out=by_row(lv["s4"]), in_=lv["t"], func=ACT.Square, scale=2.0)
+            nc.scalar.activation(out=lv["q"][:], in_=lv["s4"][:], func=ACT.Square, bias=shifts[:, 0:1])
+            nc.scalar.activation(out=lv["sq5"][:], in_=lv["s4"][:], func=ACT.Square, bias=shifts[:, 1:2])
+
+        def even_planes(u):
+            lv = live[u]
+            nc.scalar.copy(out=by_row(lv[1]), in_=lv["t"])
+            send(u, 1)
+            nc.scalar.activation(out=lv[4][:], in_=lv["q"][:], func=ACT.Identity, scale=0.5, bias=shifts[:, 2:3])
+            send(u, 4)
+            nc.scalar.activation(out=lv[2][:], in_=lv["s4"][:], func=ACT.Identity, scale=0.5, bias=shifts[:, 2:3])
+            send(u, 2)
+
+        def planes_3_5(u):
+            lv = live[u]
+            lv["t3"] = work.tile([P, CH], F32, name="t3")
+            nc.vector.scalar_tensor_tensor(
+                out=by_row(lv["t3"]), in0=by_row(lv["s4"]), scalar=3.0, in1=lv["t"], op0=ALU.subtract, op1=ALU.mult
+            )
+            nc.vector.scalar_tensor_tensor(
+                out=by_row(lv[5]), in0=by_row(lv["sq5"]), scalar=1.25, in1=lv["t"], op0=ALU.subtract, op1=ALU.mult
+            )
+            send(u, 5)
+
+        def planes_3_6(u):
+            lv = live[u]
+            lv["r6"] = work.tile([P, CH], F32, name="r6")
+            nc.scalar.activation(out=lv["r6"][:], in_=lv["t3"][:], func=ACT.Square)
+            nc.scalar.copy(out=lv[3][:], in_=lv["t3"][:])
+            send(u, 3)
+            nc.scalar.activation(out=lv[6][:], in_=lv["r6"][:], func=ACT.Identity, scale=2.0, bias=shifts[:, 2:3])
+            send(u, 6)
+
+        def product_7(u):
+            lv = live[u]
+            lv["p7"] = work.tile([P, CH], F32, name="p7")
+            nc.vector.scalar_tensor_tensor(
+                out=lv["p7"][:], in0=lv["q"][:], scalar=2.0, in1=lv["t3"][:], op0=ALU.subtract, op1=ALU.mult
+            )
+
+        def plane_7(u):
+            lv = live[u]
+            nc.vector.tensor_tensor(out=by_row(lv[7]), in0=by_row(lv["p7"]), in1=lv["t"], op=ALU.subtract)
+            send(u, 7)
+
+        def quantise(u, half):
+            cd = cpool.tile([P, 4 * P], U32, name="cod", align_bytes=64)
+            sc = cpool.tile([P, 4 * P], U8, name="scl", align_bytes=64)
+            live[u]["codes", half] = (cd, sc)
+            nc.vector.quantize_mx(
+                out=cd[:].bitcast(FP8X4),
+                scales=sc[:],
+                in_=l2s[u % L2_BUFS][:, half * 4 * CH : (half + 1) * 4 * CH],
+            )
+
+        def multiply(u, half):
+            cd, sc = live[u]["codes", half]
+            for pr in range(2):
                 po = ops.tile([P, 2, N_OUT], F32, name="po")
+                live[u]["po", half, pr] = po
                 for e in range(2):
-                    t = pr * 2 + e
+                    b = pr * 2 + e
                     nc.tensor.matmul_mx(
                         out=po[:, e, :],
-                        lhsT=cd[:, t * P : (t + 1) * P].bitcast(FP8X4),
-                        lhsT_scale=sc[:, t * P : (t + 1) * P],
+                        lhsT=cd[:, b * P : (b + 1) * P].bitcast(FP8X4),
+                        lhsT_scale=sc[:, b * P : (b + 1) * P],
                         rhs=w_codes[:].bitcast(FP8X4),
                         rhs_scale=w_scales[:],
                         start=True,
                         stop=True,
                     )
-                nc.vector.tensor_tensor(out=ob[:, pr * 2 : pr * 2 + 2, :], in0=po[:], in1=bias_f[:], op=ALU.add)
-                if u == len(UNITS) - 1:
-                    nc.sync.dma_start(
-                        out=out_rows[:, starts[u] + pr * 2 : starts[u] + pr * 2 + 2, :], in_=ob[:, pr * 2 : pr * 2 + 2, :]
-                    )
-            if u < len(UNITS) - 1:
-                nc.sync.dma_start(out=out_rows[:, starts[u] : starts[u] + n, :], in_=ob[:, 0:n, :])
 
-        n_units = len(UNITS)
-        for step in range(n_units + 3):
-            if step < n_units:
-                gen(step)
-            if 0 <= step - 2 < n_units:
-                turn(step - 2)
-            if 0 <= step - 3 < n_units:
-                multiply(step - 3)
+        def finish(u, half):
+            ob = outp.tile([P, 4, N_OUT], F32, name="ob")
+            for pr in range(2):
+                nc.vector.tensor_tensor(
+                    out=ob[:, pr * 2 : pr * 2 + 2, :], in0=live[u]["po", half, pr][:], in1=bias_f[:], op=ALU.add
+                )
+            t_out = u * TB + half * 4
+            nc.sync.dma_start(out=out_rows[:, t_out : t_out + 4, :], in_=ob[:])
+
+        def ok(u):
+            return 0 <= u < n_units
+
+        ctx.enter_context(tc.manual_schedule())
+        turn(0)
+        for s in range(n_units + LAG):
+            if ok(s - 1):
+                planes_3_5(s - 1)
+            if ok(s):
+                squares(s)
+            if ok(s - LAG):
+                quantise(s - LAG, 0)
+                multiply(s - LAG, 0)
+            if ok(s - 1):
+                planes_3_6(s - 1)
+                product_7(s - 1)
+            if ok(s - LAG):
+                quantise(s - LAG, 1)
+                multiply(s - LAG, 1)
+            if ok(s - 1):
+                plane_7(s - 1)
+            if ok(s + 1):
+                turn(s + 1)
+            if ok(s - LAG):
+                finish(s - LAG, 0)
+            if ok(s):
+                even_planes(s)
+            if ok(s - LAG):
+                finish(s - LAG, 1)

@@ -136,9 +136,13 @@ def tile_cfkanlayer_t_kernel(tc, x, cheby_coeffs, bias, out):
             lv = live[u]
             nc.scalar.copy(out=by_row(lv[1]), in_=lv["t"])
             send(u, 1)
-            nc.scalar.activation(out=lv[4][:], in_=lv["q"][:], func=ACT.Identity, scale=0.5, bias=shifts[:, 2:3])
+            nc.gpsimd.tensor_scalar(
+                out=lv[4][:], in0=lv["q"][:], scalar1=0.5, scalar2=-1.0, op0=ALU.mult, op1=ALU.add
+            )
             send(u, 4)
-            nc.scalar.activation(out=lv[2][:], in_=lv["s4"][:], func=ACT.Identity, scale=0.5, bias=shifts[:, 2:3])
+            nc.gpsimd.tensor_scalar(
+                out=lv[2][:], in0=lv["s4"][:], scalar1=0.5, scalar2=-1.0, op0=ALU.mult, op1=ALU.add
+            )
             send(u, 2)
 
         def planes_3_5(u):

@@ -22,6 +22,33 @@ CH = P * 4
 X_CHUNKS = (8, 24, 32, 64)
 L2_BUFS = 5
 LAG = 3
+STEP = (
+    ("tanh", -1),
+    ("turn", -1),
+    ("t3", 1),
+    ("s4", 0),
+    ("e10", 4),
+    ("r6", 1),
+    ("x11", 4),
+    ("t5", 1),
+    ("q", 0),
+    ("q0", 3),
+    ("m0", 3),
+    ("p7", 1),
+    ("t3b", 1),
+    ("sq5", 0),
+    ("q1", 3),
+    ("m1", 3),
+    ("t6", 1),
+    ("t7", 1),
+    ("st1", 4),
+    ("t1", 0),
+    ("e00", 3),
+    ("t4", 0),
+    ("e01", 3),
+    ("t2", 0),
+    ("st0", 3),
+)
 
 
 def tile_cfkanlayer_t_kernel(tc, x, cheby_coeffs, bias, out):
@@ -103,78 +130,100 @@ def tile_cfkanlayer_t_kernel(tc, x, cheby_coeffs, bias, out):
         def by_row(tile):
             return tile[:].rearrange("q (p i) -> q p i", i=4)
 
+        def new(u, key, dtype=F32):
+            live[u][key] = work.tile([P, CH], dtype, name="w_%s" % key)
+            return live[u][key]
+
         def send(u, k):
             nc.sync.dma_start(out=l2s[u % L2_BUFS][k:P:8, :], in_=live[u][k][:])
 
-        def turn(u):
-            lv = {}
-            live[u] = lv
-            for k in range(1, N_DEG):
-                lv[k] = work.tile([P, CH], BF16, name="pl%d" % k)
-            tr = work.tile([P, CH], F32, name="tr")
+        def tanh(u):
+            live[u] = {}
+            new(u, "tr")
             xt, j = x_of_block[u * TB]
             nc.scalar.activation(
-                out=tr[:].rearrange("p (i g t) -> p g t i", i=4, t=TB),
+                out=live[u]["tr"][:].rearrange("p (i g t) -> p g t i", i=4, t=TB),
                 in_=xt[:, j * D_IN : (j + TB) * D_IN].rearrange("p (t g i) -> p g t i", t=TB, i=4),
                 func=ACT.Tanh,
             )
+
+        def turn(u):
             ps = tps.tile([P, CH], F32, name="tp", tag="tp")
             for i in range(4):
-                nc.tensor.transpose(out=ps[:, i * P : (i + 1) * P], in_=tr[:, i * P : (i + 1) * P], identity=ident[:])
-            lv["t"] = ps[:].rearrange("q (i p) -> q p i", i=4)
+                nc.tensor.transpose(
+                    out=ps[:, i * P : (i + 1) * P], in_=live[u]["tr"][:, i * P : (i + 1) * P], identity=ident[:]
+                )
+            live[u]["t"] = ps[:].rearrange("q (i p) -> q p i", i=4)
 
-        def squares(u):
-            lv = live[u]
-            lv["s4"] = work.tile([P, CH], F32, name="s4")
-            lv["q"] = work.tile([P, CH], F32, name="q")
-            lv["sq5"] = work.tile([P, CH], F32, name="sq5")
-            nc.scalar.activation(out=by_row(lv["s4"]), in_=lv["t"], func=ACT.Square, scale=2.0)
-            nc.scalar.activation(out=lv["q"][:], in_=lv["s4"][:], func=ACT.Square, bias=shifts[:, 0:1])
-            nc.scalar.activation(out=lv["sq5"][:], in_=lv["s4"][:], func=ACT.Square, bias=shifts[:, 1:2])
+        def s4(u):
+            nc.scalar.activation(out=by_row(new(u, "s4")), in_=live[u]["t"], func=ACT.Square, scale=2.0)
 
-        def even_planes(u):
-            lv = live[u]
-            nc.scalar.copy(out=by_row(lv[1]), in_=lv["t"])
+        def q(u):
+            nc.scalar.activation(out=new(u, "q")[:], in_=live[u]["s4"][:], func=ACT.Square, bias=shifts[:, 0:1])
+
+        def sq5(u):
+            nc.scalar.activation(out=new(u, "sq5")[:], in_=live[u]["s4"][:], func=ACT.Square, bias=shifts[:, 1:2])
+
+        def t1(u):
+            nc.scalar.copy(out=by_row(new(u, 1, BF16)), in_=live[u]["t"])
             send(u, 1)
-            nc.gpsimd.tensor_scalar(
-                out=lv[4][:], in0=lv["q"][:], scalar1=0.5, scalar2=-1.0, op0=ALU.mult, op1=ALU.add
-            )
-            send(u, 4)
-            nc.gpsimd.tensor_scalar(
-                out=lv[2][:], in0=lv["s4"][:], scalar1=0.5, scalar2=-1.0, op0=ALU.mult, op1=ALU.add
-            )
-            send(u, 2)
 
-        def planes_3_5(u):
-            lv = live[u]
-            lv["t3"] = work.tile([P, CH], F32, name="t3")
-            nc.vector.scalar_tensor_tensor(
-                out=by_row(lv["t3"]), in0=by_row(lv["s4"]), scalar=3.0, in1=lv["t"], op0=ALU.subtract, op1=ALU.mult
+        def halved(u, k, src):
+            nc.gpsimd.tensor_scalar(
+                out=new(u, k, BF16)[:], in0=live[u][src][:], scalar1=0.5, scalar2=-1.0, op0=ALU.mult, op1=ALU.add
             )
+            send(u, k)
+
+        def t2(u):
+            halved(u, 2, "s4")
+
+        def t4(u):
+            halved(u, 4, "q")
+
+        def times_t(u, out_tile, src, shift):
             nc.vector.scalar_tensor_tensor(
-                out=by_row(lv[5]), in0=by_row(lv["sq5"]), scalar=1.25, in1=lv["t"], op0=ALU.subtract, op1=ALU.mult
+                out=by_row(out_tile),
+                in0=by_row(live[u][src]),
+                scalar=shift,
+                in1=live[u]["t"],
+                op0=ALU.subtract,
+                op1=ALU.mult,
             )
+
+        def t3(u):
+            times_t(u, new(u, "t3"), "s4", 3.0)
+
+        def t5(u):
+            times_t(u, new(u, 5, BF16), "sq5", 1.25)
             send(u, 5)
 
-        def planes_3_6(u):
-            lv = live[u]
-            lv["r6"] = work.tile([P, CH], F32, name="r6")
-            nc.scalar.activation(out=lv["r6"][:], in_=lv["t3"][:], func=ACT.Square)
-            nc.scalar.copy(out=lv[3][:], in_=lv["t3"][:])
+        def r6(u):
+            nc.scalar.activation(out=new(u, "r6")[:], in_=live[u]["t3"][:], func=ACT.Square)
+
+        def t3b(u):
+            nc.scalar.copy(out=new(u, 3, BF16)[:], in_=live[u]["t3"][:])
             send(u, 3)
-            nc.scalar.activation(out=lv[6][:], in_=lv["r6"][:], func=ACT.Identity, scale=2.0, bias=shifts[:, 2:3])
+
+        def t6(u):
+            nc.scalar.activation(
+                out=new(u, 6, BF16)[:], in_=live[u]["r6"][:], func=ACT.Identity, scale=2.0, bias=shifts[:, 2:3]
+            )
             send(u, 6)
 
-        def product_7(u):
-            lv = live[u]
-            lv["p7"] = work.tile([P, CH], F32, name="p7")
+        def p7(u):
             nc.vector.scalar_tensor_tensor(
-                out=lv["p7"][:], in0=lv["q"][:], scalar=2.0, in1=lv["t3"][:], op0=ALU.subtract, op1=ALU.mult
+                out=new(u, "p7")[:],
+                in0=live[u]["q"][:],
+                scalar=2.0,
+                in1=live[u]["t3"][:],
+                op0=ALU.subtract,
+                op1=ALU.mult,
             )
 
-        def plane_7(u):
-            lv = live[u]
-            nc.vector.tensor_tensor(out=by_row(lv[7]), in0=by_row(lv["p7"]), in1=lv["t"], op=ALU.subtract)
+        def t7(u):
+            nc.vector.tensor_tensor(
+                out=by_row(new(u, 7, BF16)), in0=by_row(live[u]["p7"]), in1=live[u]["t"], op=ALU.subtract
+            )
             send(u, 7)
 
         def quantise(u, half):
@@ -187,8 +236,15 @@ def tile_cfkanlayer_t_kernel(tc, x, cheby_coeffs, bias, out):
                 in_=l2s[u % L2_BUFS][:, half * 4 * CH : (half + 1) * 4 * CH],
             )
 
+        def q0(u):
+            quantise(u, 0)
+
+        def q1(u):
+            quantise(u, 1)
+
         def multiply(u, half):
             cd, sc = live[u]["codes", half]
+            live[u]["ob", half] = outp.tile([P, 4, N_OUT], F32, name="ob")
             for pr in range(2):
                 po = ops.tile([P, 2, N_OUT], F32, name="po")
                 live[u]["po", half, pr] = po
@@ -204,41 +260,49 @@ def tile_cfkanlayer_t_kernel(tc, x, cheby_coeffs, bias, out):
                         stop=True,
                     )
 
-        def finish(u, half):
-            ob = outp.tile([P, 4, N_OUT], F32, name="ob")
-            for pr in range(2):
-                nc.vector.tensor_tensor(
-                    out=ob[:, pr * 2 : pr * 2 + 2, :], in0=live[u]["po", half, pr][:], in1=bias_f[:], op=ALU.add
-                )
-            t_out = u * TB + half * 4
-            nc.sync.dma_start(out=out_rows[:, t_out : t_out + 4, :], in_=ob[:])
+        def m0(u):
+            multiply(u, 0)
 
-        def ok(u):
-            return 0 <= u < n_units
+        def m1(u):
+            multiply(u, 1)
+
+        def evac(u, half, pr):
+            dst = live[u]["ob", half][:, pr * 2 : pr * 2 + 2, :]
+            nc.vector.tensor_tensor(out=dst, in0=live[u]["po", half, pr][:], in1=bias_f[:], op=ALU.add)
+
+        def e00(u):
+            evac(u, 0, 0)
+
+        def e01(u):
+            evac(u, 0, 1)
+
+        def e10(u):
+            evac(u, 1, 0)
+
+        def e11(u):
+            evac(u, 1, 1)
+
+        def x11(u):
+            raw = outp.tile([P, 2, N_OUT], F32, name="raw")
+            dst = live[u]["ob", 1][:, 2:4, :]
+            nc.scalar.copy(out=raw[:], in_=live[u]["po", 1, 1][:])
+            nc.gpsimd.tensor_tensor(out=dst, in0=raw[:], in1=bias_f[:], op=ALU.add)
+
+        def store(u, half):
+            t_out = u * TB + half * 4
+            nc.sync.dma_start(out=out_rows[:, t_out : t_out + 4, :], in_=live[u]["ob", half][:])
+
+        def st0(u):
+            store(u, 0)
+
+        def st1(u):
+            store(u, 1)
 
         ctx.enter_context(tc.manual_schedule())
+        tanh(0)
         turn(0)
-        for s in range(n_units + LAG):
-            if ok(s - 1):
-                planes_3_5(s - 1)
-            if ok(s):
-                squares(s)
-            if ok(s - LAG):
-                quantise(s - LAG, 0)
-                multiply(s - LAG, 0)
-            if ok(s - 1):
-                planes_3_6(s - 1)
-                product_7(s - 1)
-            if ok(s - LAG):
-                quantise(s - LAG, 1)
-                multiply(s - LAG, 1)
-            if ok(s - 1):
-                plane_7(s - 1)
-            if ok(s + 1):
-                turn(s + 1)
-            if ok(s - LAG):
-                finish(s - LAG, 0)
-            if ok(s):
-                even_planes(s)
-            if ok(s - LAG):
-                finish(s - LAG, 1)
+        for s in range(n_units + LAG + 2):
+            for work_of, lag in STEP:
+                if 0 <= s - lag < n_units and not (lag == -1 and s == -1):
+                    work_of_unit = {"tanh": tanh, "turn": turn, "s4": s4, "q": q, "sq5": sq5, "t1": t1, "t2": t2, "t4": t4, "t3": t3, "t5": t5, "r6": r6, "t3b": t3b, "t6": t6, "p7": p7, "t7": t7, "q0": q0, "q1": q1, "m0": m0, "m1": m1, "e00": e00, "e01": e01, "e10": e10, "e11": e11, "x11": x11, "st0": st0, "st1": st1}[work_of]
+                    work_of_unit(s - lag)

@@ -21,7 +21,13 @@ TB = 8
 CH = P * 4
 X_CHUNKS = (8, 24, 32, 64)
 L2_BUFS = 5
-LAG = 3
+LAG = 4
+PLACE = (0, 1, 2, 3, 4, 5, 6, 7)
+ACT_SENDS = ()
+EARLY = 3
+W_STEP = 0
+T3G = False
+T6G = False
 STEP = (
     ("tanh", -1),
     ("turn", -1),
@@ -29,26 +35,37 @@ STEP = (
     ("s4", 0),
     ("e10", 4),
     ("r6", 1),
-    ("x11", 4),
     ("t5", 1),
+    ("d5", 1),
     ("q", 0),
     ("q0", 3),
     ("m0", 3),
-    ("p7", 1),
     ("t3b", 1),
+    ("d3", 1),
+    ("p7", 1),
     ("sq5", 0),
     ("q1", 3),
     ("m1", 3),
-    ("t6", 1),
-    ("t7", 1),
-    ("st1", 4),
-    ("t1", 0),
-    ("e00", 3),
-    ("t4", 0),
-    ("e01", 3),
+    ("e11", 4),
     ("t2", 0),
+    ("t4", 0),
+    ("t7", 1),
+    ("d7", 1),
+    ("st1", 4),
+    ("t6", 1),
+    ("d6", 1),
+    ("t1", 0),
+    ("d1", 0),
+    ("e00", 3),
+    ("d4", 0),
+    ("e01", 3),
+    ("d2", 0),
     ("st0", 3),
 )
+
+
+def ON_SCALAR(u, half, pr):
+    return (half, pr) == (1, 1) and u < 15
 
 
 def tile_cfkanlayer_t_kernel(tc, x, cheby_coeffs, bias, out):
@@ -92,37 +109,38 @@ def tile_cfkanlayer_t_kernel(tc, x, cheby_coeffs, bias, out):
             nc.sync.dma_start(out=l2[0:P:8, :], in_=ones[:])
             l2s.append(l2)
 
-        w_re = const.tile([P, 2, K_ALL], BF16, name="w_re")
-        for h in range(2):
-            nc.vector.tensor_copy(
-                out=w_re[:, h, :].rearrange("p (i g k) -> p i g k", i=4, k=N_DEG),
-                in_=w_raw[:, h, :].rearrange("p (g i k) -> p i g k", i=4, k=N_DEG),
-            )
-        w_grp = const.tile([P, N_OUT, 4], BF16, name="w_grp", align_bytes=64)
-        for h in range(2):
-            w_ps = tps.tile([P, 4 * P], BF16, name="w_ps", tag="tp")
-            for i in range(4):
-                nc.tensor.transpose(
-                    out=w_ps[:, i * P : (i + 1) * P],
-                    in_=w_re[:, h, i * P : (i + 1) * P],
-                    identity=ident_bf[:],
-                )
-            nc.vector.tensor_copy(
-                out=w_grp[:, h * P : (h + 1) * P, :],
-                in_=w_ps[:].rearrange("p (i o) -> p o i", i=4),
-            )
-        w_codes = const.tile([P, N_OUT], U32, name="w_codes", align_bytes=64)
-        w_scales = const.tile([P, N_OUT], U8, name="w_scales", align_bytes=64)
-        nc.vector.quantize_mx(
-            out=w_codes[:].bitcast(FP8X4),
-            scales=w_scales[:],
-            in_=w_grp[:].rearrange("p o a -> p (o a)"),
-        )
-        bias_f = const.tile([P, 2, N_OUT], F32, name="bias_f")
-        nc.vector.tensor_copy(out=bias_f[:, 0, :], in_=bias_bf[:])
-        nc.vector.tensor_copy(out=bias_f[:, 1, :], in_=bias_bf[:])
-
         out_rows = out.rearrange("(p t) o -> p t o", t=NB)
+
+        def prepare_weights():
+            w_re = const.tile([P, 2, K_ALL], BF16, name="w_re")
+            w_dst = w_re[:].rearrange("p h (i g k) -> p h i g k", i=4, k=N_DEG)
+            w_src = w_raw[:].rearrange("p h (g i k) -> p h i g k", i=4, k=N_DEG)
+            for h in range(2):
+                nc.vector.tensor_copy(out=w_dst[:, h], in_=w_src[:, h])
+            w_grp = const.tile([P, N_OUT, 4], BF16, name="w_grp", align_bytes=64)
+            for h in range(2):
+                w_ps = tps.tile([P, 4 * P], BF16, name="w_ps", tag="tp")
+                for i in range(4):
+                    nc.tensor.transpose(
+                        out=w_ps[:, i * P : (i + 1) * P],
+                        in_=w_re[:, h, i * P : (i + 1) * P],
+                        identity=ident_bf[:],
+                    )
+                nc.vector.tensor_copy(
+                    out=w_grp[:, h * P : (h + 1) * P, :],
+                    in_=w_ps[:].rearrange("p (i o) -> p o i", i=4),
+                )
+            w_codes = const.tile([P, N_OUT], U32, name="w_codes", align_bytes=64)
+            w_scales = const.tile([P, N_OUT], U8, name="w_scales", align_bytes=64)
+            nc.vector.quantize_mx(
+                out=w_codes[:].bitcast(FP8X4),
+                scales=w_scales[:],
+                in_=w_grp[:].rearrange("p o a -> p (o a)"),
+            )
+            bias_f = const.tile([P, 2, N_OUT], F32, name="bias_f")
+            nc.vector.tensor_copy(out=bias_f[:, 0, :], in_=bias_bf[:])
+            nc.vector.tensor_copy(out=bias_f[:, 1, :], in_=bias_bf[:])
+            return w_codes, w_scales, bias_f
 
         live = {}
         n_units = NB // TB
@@ -135,7 +153,8 @@ def tile_cfkanlayer_t_kernel(tc, x, cheby_coeffs, bias, out):
             return live[u][key]
 
         def send(u, k):
-            nc.sync.dma_start(out=l2s[u % L2_BUFS][k:P:8, :], in_=live[u][k][:])
+            eng = nc.scalar if k in ACT_SENDS else nc.sync
+            eng.dma_start(out=l2s[u % L2_BUFS][PLACE[k] : P : 8, :], in_=live[u][k][:])
 
         def tanh(u):
             live[u] = {}
@@ -166,13 +185,11 @@ def tile_cfkanlayer_t_kernel(tc, x, cheby_coeffs, bias, out):
 
         def t1(u):
             nc.scalar.copy(out=by_row(new(u, 1, BF16)), in_=live[u]["t"])
-            send(u, 1)
 
         def halved(u, k, src):
             nc.gpsimd.tensor_scalar(
                 out=new(u, k, BF16)[:], in0=live[u][src][:], scalar1=0.5, scalar2=-1.0, op0=ALU.mult, op1=ALU.add
             )
-            send(u, k)
 
         def t2(u):
             halved(u, 2, "s4")
@@ -195,20 +212,28 @@ def tile_cfkanlayer_t_kernel(tc, x, cheby_coeffs, bias, out):
 
         def t5(u):
             times_t(u, new(u, 5, BF16), "sq5", 1.25)
-            send(u, 5)
 
         def r6(u):
             nc.scalar.activation(out=new(u, "r6")[:], in_=live[u]["t3"][:], func=ACT.Square)
 
         def t3b(u):
-            nc.scalar.copy(out=new(u, 3, BF16)[:], in_=live[u]["t3"][:])
-            send(u, 3)
+            dst = new(u, 3, BF16)[:]
+            src = live[u]["t3"][:]
+            if u < EARLY:
+                nc.vector.tensor_copy(out=dst, in_=src)
+            elif T3G:
+                nc.gpsimd.tensor_scalar(out=dst, in0=src, scalar1=1.0, scalar2=0.0, op0=ALU.mult, op1=ALU.add)
+            else:
+                nc.scalar.copy(out=dst, in_=src)
 
         def t6(u):
-            nc.scalar.activation(
-                out=new(u, 6, BF16)[:], in_=live[u]["r6"][:], func=ACT.Identity, scale=2.0, bias=shifts[:, 2:3]
-            )
-            send(u, 6)
+            dst = new(u, 6, BF16)[:]
+            src = live[u]["r6"][:]
+            if u < EARLY or T6G:
+                eng = nc.vector if u < EARLY else nc.gpsimd
+                eng.tensor_scalar(out=dst, in0=src, scalar1=2.0, scalar2=-1.0, op0=ALU.mult, op1=ALU.add)
+            else:
+                nc.scalar.activation(out=dst, in_=src, func=ACT.Identity, scale=2.0, bias=shifts[:, 2:3])
 
         def p7(u):
             nc.vector.scalar_tensor_tensor(
@@ -224,7 +249,6 @@ def tile_cfkanlayer_t_kernel(tc, x, cheby_coeffs, bias, out):
             nc.vector.tensor_tensor(
                 out=by_row(new(u, 7, BF16)), in0=by_row(live[u]["p7"]), in1=live[u]["t"], op=ALU.subtract
             )
-            send(u, 7)
 
         def quantise(u, half):
             cd = cpool.tile([P, 4 * P], U32, name="cod", align_bytes=64)
@@ -235,12 +259,6 @@ def tile_cfkanlayer_t_kernel(tc, x, cheby_coeffs, bias, out):
                 scales=sc[:],
                 in_=l2s[u % L2_BUFS][:, half * 4 * CH : (half + 1) * 4 * CH],
             )
-
-        def q0(u):
-            quantise(u, 0)
-
-        def q1(u):
-            quantise(u, 1)
 
         def multiply(u, half):
             cd, sc = live[u]["codes", half]
@@ -260,49 +278,39 @@ def tile_cfkanlayer_t_kernel(tc, x, cheby_coeffs, bias, out):
                         stop=True,
                     )
 
-        def m0(u):
-            multiply(u, 0)
-
-        def m1(u):
-            multiply(u, 1)
-
         def evac(u, half, pr):
             dst = live[u]["ob", half][:, pr * 2 : pr * 2 + 2, :]
-            nc.vector.tensor_tensor(out=dst, in0=live[u]["po", half, pr][:], in1=bias_f[:], op=ALU.add)
-
-        def e00(u):
-            evac(u, 0, 0)
-
-        def e01(u):
-            evac(u, 0, 1)
-
-        def e10(u):
-            evac(u, 1, 0)
-
-        def e11(u):
-            evac(u, 1, 1)
-
-        def x11(u):
-            raw = outp.tile([P, 2, N_OUT], F32, name="raw")
-            dst = live[u]["ob", 1][:, 2:4, :]
-            nc.scalar.copy(out=raw[:], in_=live[u]["po", 1, 1][:])
-            nc.gpsimd.tensor_tensor(out=dst, in0=raw[:], in1=bias_f[:], op=ALU.add)
+            po = live[u]["po", half, pr]
+            if ON_SCALAR(u, half, pr):
+                raw = outp.tile([P, 2, N_OUT], F32, name="raw")
+                nc.scalar.copy(out=raw[:], in_=po[:])
+                nc.gpsimd.tensor_tensor(out=dst, in0=raw[:], in1=bias_f[:], op=ALU.add)
+            else:
+                nc.vector.tensor_tensor(out=dst, in0=po[:], in1=bias_f[:], op=ALU.add)
 
         def store(u, half):
             t_out = u * TB + half * 4
             nc.sync.dma_start(out=out_rows[:, t_out : t_out + 4, :], in_=live[u]["ob", half][:])
 
-        def st0(u):
-            store(u, 0)
-
-        def st1(u):
-            store(u, 1)
-
+        OPS = {
+            "tanh": tanh, "turn": turn, "s4": s4, "q": q, "sq5": sq5, "t1": t1, "t2": t2, "t3": t3, "t3b": t3b, "t4": t4,
+            "t5": t5, "r6": r6, "t6": t6, "p7": p7, "t7": t7,
+            "q0": lambda u: quantise(u, 0), "q1": lambda u: quantise(u, 1),
+            "m0": lambda u: multiply(u, 0), "m1": lambda u: multiply(u, 1),
+            "e00": lambda u: evac(u, 0, 0), "e01": lambda u: evac(u, 0, 1),
+            "e10": lambda u: evac(u, 1, 0), "e11": lambda u: evac(u, 1, 1),
+            "st0": lambda u: store(u, 0), "st1": lambda u: store(u, 1),
+            "d1": lambda u: send(u, 1), "d2": lambda u: send(u, 2), "d3": lambda u: send(u, 3), "d4": lambda u: send(u, 4),
+            "d5": lambda u: send(u, 5), "d6": lambda u: send(u, 6), "d7": lambda u: send(u, 7),
+        }
         ctx.enter_context(tc.manual_schedule())
         tanh(0)
         turn(0)
-        for s in range(n_units + LAG + 2):
-            for work_of, lag in STEP:
-                if 0 <= s - lag < n_units and not (lag == -1 and s == -1):
-                    work_of_unit = {"tanh": tanh, "turn": turn, "s4": s4, "q": q, "sq5": sq5, "t1": t1, "t2": t2, "t4": t4, "t3": t3, "t5": t5, "r6": r6, "t3b": t3b, "t6": t6, "p7": p7, "t7": t7, "q0": q0, "q1": q1, "m0": m0, "m1": m1, "e00": e00, "e01": e01, "e10": e10, "e11": e11, "x11": x11, "st0": st0, "st1": st1}[work_of]
-                    work_of_unit(s - lag)
+        w_codes = w_scales = bias_f = None
+        for s in range(n_units + LAG):
+            for name, lag in STEP:
+                u = s - lag
+                if 0 <= u < n_units:
+                    OPS[name](u)
+            if s == W_STEP:
+                w_codes, w_scales, bias_f = prepare_weights()

@@ -24,10 +24,57 @@ L2_BUFS = 5
 LAG = 4
 PLACE = (0, 1, 2, 3, 4, 5, 6, 7)
 ACT_SENDS = ()
-EARLY = 3
+EARLY = 2
 W_STEP = 0
+W_AFTER = "st0"
 T3G = False
 T6G = False
+TAIL = (
+    ("t3", 15),
+    ("e10", 12),
+    ("r6", 15),
+    ("t5", 15),
+    ("d5", 15),
+    ("q0", 13),
+    ("m0", 13),
+    ("t3b", 15),
+    ("d3", 15),
+    ("p7", 15),
+    ("q1", 13),
+    ("e11", 12),
+    ("m1", 13),
+    ("t6", 15),
+    ("d6", 15),
+    ("t7", 15),
+    ("d7", 15),
+    ("st1", 12),
+    ("q0", 14),
+    ("e00", 13),
+    ("e01", 13),
+    ("m0", 14),
+    ("st0", 13),
+    ("q1", 14),
+    ("e10", 13),
+    ("e11", 13),
+    ("m1", 14),
+    ("st1", 13),
+    ("e00", 14),
+    ("q0", 15),
+    ("e01", 14),
+    ("m0", 15),
+    ("st0", 14),
+    ("q1", 15),
+    ("e10", 14),
+    ("e11", 14),
+    ("m1", 15),
+    ("st1", 14),
+    ("e00", 15),
+    ("e01", 15),
+    ("st0", 15),
+    ("e10", 15),
+    ("e11", 15),
+    ("st1", 15),
+)
 STEP = (
     ("tanh", -1),
     ("turn", -1),
@@ -49,13 +96,13 @@ STEP = (
     ("e11", 4),
     ("t2", 0),
     ("t4", 0),
+    ("t6", 1),
     ("t7", 1),
     ("d7", 1),
     ("st1", 4),
-    ("t6", 1),
-    ("d6", 1),
     ("t1", 0),
     ("d1", 0),
+    ("d6", 1),
     ("e00", 3),
     ("d4", 0),
     ("e01", 3),
@@ -65,7 +112,7 @@ STEP = (
 
 
 def ON_SCALAR(u, half, pr):
-    return (half, pr) == (1, 1) and u < 15
+    return (half, pr) == (1, 1) and u < 14 or (half, pr, u) in ((0, 1, 14),)
 
 
 def tile_cfkanlayer_t_kernel(tc, x, cheby_coeffs, bias, out):
@@ -79,30 +126,35 @@ def tile_cfkanlayer_t_kernel(tc, x, cheby_coeffs, bias, out):
         tps = ctx.enter_context(tc.psum_pool(name="tps", bufs=4))
         ops = ctx.enter_context(tc.psum_pool(name="ops", bufs=4))
 
+        ident = const.tile([P, P], F32, name="ident")
+        make_identity(nc, ident[:])
         x_rows = x.rearrange("(p t) d -> p (t d)", t=NB)
         x_of_block = []
-        first = 0
-        for ci, n_blocks in enumerate(X_CHUNKS):
-            xt = const.tile([P, n_blocks * D_IN], BF16, name="x%d" % ci)
+
+        def load_x(n_blocks):
+            first = len(x_of_block)
+            xt = const.tile([P, n_blocks * D_IN], BF16, name="x%d" % first)
             nc.sync.dma_start(out=xt[:], in_=x_rows[:, first * D_IN : (first + n_blocks) * D_IN])
             for j in range(n_blocks):
                 x_of_block.append((xt, j))
-            first += n_blocks
-        w_raw = const.tile([P, 2, K_ALL], BF16, name="w_raw")
-        nc.scalar.dma_start(out=w_raw[:], in_=cheby_coeffs.rearrange("(h p) d k -> p h (d k)", p=P))
-        bias_bf = const.tile([P, N_OUT], BF16, name="bias_bf")
-        nc.gpsimd.dma_start(out=bias_bf[:], in_=bias.rearrange("o n -> (o n)").partition_broadcast(P))
 
-        ident = const.tile([P, P], F32, name="ident")
-        make_identity(nc, ident[:])
-        ident_bf = const.tile([P, P], BF16, name="ident_bf")
-        nc.vector.tensor_copy(out=ident_bf[:], in_=ident[:])
+        load_x(X_CHUNKS[0])
+        w_raw = const.tile([P, 2, K_ALL], BF16, name="w_raw")
+        nc.sync.dma_start(out=w_raw[:], in_=cheby_coeffs.rearrange("(h p) d k -> p h (d k)", p=P))
+        for n_blocks in X_CHUNKS[1:]:
+            load_x(n_blocks)
+
         shifts = const.tile([P, 3], F32, name="shifts")
         nc.vector.memset(shifts[:, 0:1], -2.0)
         nc.vector.memset(shifts[:, 1:2], -2.5)
         nc.vector.memset(shifts[:, 2:3], -1.0)
+        bias_row = const.tile([P, N_OUT], BF16, name="bias_row")
+        nc.vector.memset(bias_row[:], 0.0)
+        nc.gpsimd.dma_start(out=bias_row[0:1, :], in_=bias)
         ones = const.tile([P, CH], BF16, name="ones")
         nc.vector.memset(ones[:], 1.0)
+        ident_bf = const.tile([P, P], BF16, name="ident_bf")
+        nc.vector.tensor_copy(out=ident_bf[:], in_=ident[:])
         l2s = []
         for b in range(L2_BUFS):
             l2 = const.tile([P, TB * CH], BF16, name="l2_%d" % b, align_bytes=64)
@@ -117,6 +169,9 @@ def tile_cfkanlayer_t_kernel(tc, x, cheby_coeffs, bias, out):
             w_src = w_raw[:].rearrange("p h (g i k) -> p h i g k", i=4, k=N_DEG)
             for h in range(2):
                 nc.vector.tensor_copy(out=w_dst[:, h], in_=w_src[:, h])
+            return w_re
+
+        def turn_weights(w_re):
             w_grp = const.tile([P, N_OUT, 4], BF16, name="w_grp", align_bytes=64)
             for h in range(2):
                 w_ps = tps.tile([P, 4 * P], BF16, name="w_ps", tag="tp")
@@ -138,8 +193,10 @@ def tile_cfkanlayer_t_kernel(tc, x, cheby_coeffs, bias, out):
                 in_=w_grp[:].rearrange("p o a -> p (o a)"),
             )
             bias_f = const.tile([P, 2, N_OUT], F32, name="bias_f")
-            nc.vector.tensor_copy(out=bias_f[:, 0, :], in_=bias_bf[:])
-            nc.vector.tensor_copy(out=bias_f[:, 1, :], in_=bias_bf[:])
+            b_ps = tps.tile([P, CH], F32, name="b_ps", tag="tp")
+            nc.tensor.matmul(out=b_ps[:, 0:N_OUT], lhsT=ones[:, 0:P], rhs=bias_row[:], start=True, stop=True)
+            for e in range(2):
+                nc.vector.tensor_copy(out=bias_f[:, e, :], in_=b_ps[:, 0:N_OUT])
             return w_codes, w_scales, bias_f
 
         live = {}
@@ -290,7 +347,14 @@ def tile_cfkanlayer_t_kernel(tc, x, cheby_coeffs, bias, out):
 
         def store(u, half):
             t_out = u * TB + half * 4
-            nc.sync.dma_start(out=out_rows[:, t_out : t_out + 4, :], in_=live[u]["ob", half][:])
+            if u == n_units - 1 and half == 1:
+                for pr in range(2):
+                    nc.sync.dma_start(
+                        out=out_rows[:, t_out + pr * 2 : t_out + pr * 2 + 2, :],
+                        in_=live[u]["ob", half][:, pr * 2 : pr * 2 + 2, :],
+                    )
+            else:
+                nc.sync.dma_start(out=out_rows[:, t_out : t_out + 4, :], in_=live[u]["ob", half][:])
 
         OPS = {
             "tanh": tanh, "turn": turn, "s4": s4, "q": q, "sq5": sq5, "t1": t1, "t2": t2, "t3": t3, "t3b": t3b, "t4": t4,
@@ -304,13 +368,16 @@ def tile_cfkanlayer_t_kernel(tc, x, cheby_coeffs, bias, out):
             "d5": lambda u: send(u, 5), "d6": lambda u: send(u, 6), "d7": lambda u: send(u, 7),
         }
         ctx.enter_context(tc.manual_schedule())
+        w_re = prepare_weights()
         tanh(0)
         turn(0)
         w_codes = w_scales = bias_f = None
-        for s in range(n_units + LAG):
+        for s in range(n_units):
             for name, lag in STEP:
                 u = s - lag
                 if 0 <= u < n_units:
                     OPS[name](u)
-            if s == W_STEP:
-                w_codes, w_scales, bias_f = prepare_weights()
+                if s == W_STEP and name == W_AFTER:
+                    w_codes, w_scales, bias_f = turn_weights(w_re)
+        for name, u in TAIL:
+            OPS[name](u)

@@ -25,8 +25,7 @@ LAG = 4
 PLACE = (0, 1, 2, 3, 4, 5, 6, 7)
 ACT_SENDS = ()
 EARLY = 2
-W_STEP = 0
-W_AFTER = "st0"
+W_AT = {(0, "turn"): ("wt0", "wt1",), (1, "t5"): ("wc0",), (1, "p7"): ("wc1",), (2, "t5"): ("wq",), (2, "t7"): ("wb",)}
 T3G = False
 T6G = False
 TAIL = (
@@ -42,6 +41,7 @@ TAIL = (
     ("p7", 15),
     ("q1", 13),
     ("e11", 12),
+    ("a11", 12),
     ("m1", 13),
     ("t6", 15),
     ("d6", 15),
@@ -56,16 +56,19 @@ TAIL = (
     ("q1", 14),
     ("e10", 13),
     ("e11", 13),
+    ("a11", 13),
     ("m1", 14),
     ("st1", 13),
     ("e00", 14),
     ("q0", 15),
     ("e01", 14),
+    ("a01", 14),
     ("m0", 15),
     ("st0", 14),
     ("q1", 15),
     ("e10", 14),
     ("e11", 14),
+    ("a11", 14),
     ("m1", 15),
     ("st1", 14),
     ("e00", 15),
@@ -90,15 +93,16 @@ STEP = (
     ("t3b", 1),
     ("d3", 1),
     ("p7", 1),
+    ("e11", 4),
     ("sq5", 0),
     ("q1", 3),
     ("m1", 3),
-    ("e11", 4),
+    ("a11", 4),
     ("t2", 0),
     ("t4", 0),
-    ("t6", 1),
     ("t7", 1),
     ("d7", 1),
+    ("t6", 1),
     ("st1", 4),
     ("t1", 0),
     ("d1", 0),
@@ -150,7 +154,7 @@ def tile_cfkanlayer_t_kernel(tc, x, cheby_coeffs, bias, out):
         nc.vector.memset(shifts[:, 2:3], -1.0)
         bias_row = const.tile([P, N_OUT], BF16, name="bias_row")
         nc.vector.memset(bias_row[:], 0.0)
-        nc.gpsimd.dma_start(out=bias_row[0:1, :], in_=bias)
+        nc.sync.dma_start(out=bias_row[0:1, :], in_=bias)
         ones = const.tile([P, CH], BF16, name="ones")
         nc.vector.memset(ones[:], 1.0)
         ident_bf = const.tile([P, P], BF16, name="ident_bf")
@@ -171,34 +175,39 @@ def tile_cfkanlayer_t_kernel(tc, x, cheby_coeffs, bias, out):
                 nc.vector.tensor_copy(out=w_dst[:, h], in_=w_src[:, h])
             return w_re
 
-        def turn_weights(w_re):
-            w_grp = const.tile([P, N_OUT, 4], BF16, name="w_grp", align_bytes=64)
-            for h in range(2):
-                w_ps = tps.tile([P, 4 * P], BF16, name="w_ps", tag="tp")
-                for i in range(4):
-                    nc.tensor.transpose(
-                        out=w_ps[:, i * P : (i + 1) * P],
-                        in_=w_re[:, h, i * P : (i + 1) * P],
-                        identity=ident_bf[:],
-                    )
-                nc.vector.tensor_copy(
-                    out=w_grp[:, h * P : (h + 1) * P, :],
-                    in_=w_ps[:].rearrange("p (i o) -> p o i", i=4),
-                )
-            w_codes = const.tile([P, N_OUT], U32, name="w_codes", align_bytes=64)
-            w_scales = const.tile([P, N_OUT], U8, name="w_scales", align_bytes=64)
-            nc.vector.quantize_mx(
-                out=w_codes[:].bitcast(FP8X4),
-                scales=w_scales[:],
-                in_=w_grp[:].rearrange("p o a -> p (o a)"),
-            )
-            bias_f = const.tile([P, 2, N_OUT], F32, name="bias_f")
-            b_ps = tps.tile([P, CH], F32, name="b_ps", tag="tp")
-            nc.tensor.matmul(out=b_ps[:, 0:N_OUT], lhsT=ones[:, 0:P], rhs=bias_row[:], start=True, stop=True)
-            for e in range(2):
-                nc.vector.tensor_copy(out=bias_f[:, e, :], in_=b_ps[:, 0:N_OUT])
-            return w_codes, w_scales, bias_f
+        w_grp = const.tile([P, N_OUT, 4], BF16, name="w_grp", align_bytes=64)
+        w_codes = const.tile([P, N_OUT], U32, name="w_codes", align_bytes=64)
+        w_scales = const.tile([P, N_OUT], U8, name="w_scales", align_bytes=64)
+        bias_f = const.tile([P, 2, N_OUT], F32, name="bias_f")
+        w_turned = {}
 
+        def turn_weights(h):
+            w_turned[h] = ops.tile([P, 4 * P], BF16, name="w_ps", tag="po")
+            for i in range(4):
+                nc.tensor.transpose(
+                    out=w_turned[h][:, i * P : (i + 1) * P], in_=w_re[:, h, i * P : (i + 1) * P], identity=ident_bf[:]
+                )
+
+        def group_weights(h):
+            nc.vector.tensor_copy(
+                out=w_grp[:, h * P : (h + 1) * P, :], in_=w_turned[h][:].rearrange("p (i o) -> p o i", i=4)
+            )
+
+        def quantise_weights():
+            nc.vector.quantize_mx(
+                out=w_codes[:].bitcast(FP8X4), scales=w_scales[:], in_=w_grp[:].rearrange("p o a -> p (o a)")
+            )
+
+        def spread_bias():
+            b_ps = ops.tile([P, N_OUT], F32, name="b_ps", tag="po")
+            nc.tensor.matmul(out=b_ps[:], lhsT=ones[:, 0:P], rhs=bias_row[:], start=True, stop=True)
+            for e in range(2):
+                nc.vector.tensor_copy(out=bias_f[:, e, :], in_=b_ps[:])
+
+        W_OPS = {
+            "wt0": lambda: turn_weights(0), "wt1": lambda: turn_weights(1), "wc0": lambda: group_weights(0),
+            "wc1": lambda: group_weights(1), "wq": quantise_weights, "wb": spread_bias,
+        }
         live = {}
         n_units = NB // TB
 
@@ -321,7 +330,7 @@ def tile_cfkanlayer_t_kernel(tc, x, cheby_coeffs, bias, out):
             cd, sc = live[u]["codes", half]
             live[u]["ob", half] = outp.tile([P, 4, N_OUT], F32, name="ob")
             for pr in range(2):
-                po = ops.tile([P, 2, N_OUT], F32, name="po")
+                po = ops.tile([P, 2, N_OUT], F32, name="po", tag="po")
                 live[u]["po", half, pr] = po
                 for e in range(2):
                     b = pr * 2 + e
@@ -340,10 +349,15 @@ def tile_cfkanlayer_t_kernel(tc, x, cheby_coeffs, bias, out):
             po = live[u]["po", half, pr]
             if ON_SCALAR(u, half, pr):
                 raw = outp.tile([P, 2, N_OUT], F32, name="raw")
+                live[u]["raw", half, pr] = raw
                 nc.scalar.copy(out=raw[:], in_=po[:])
-                nc.gpsimd.tensor_tensor(out=dst, in0=raw[:], in1=bias_f[:], op=ALU.add)
             else:
                 nc.vector.tensor_tensor(out=dst, in0=po[:], in1=bias_f[:], op=ALU.add)
+
+        def add_bias(u, half, pr):
+            if ON_SCALAR(u, half, pr):
+                dst = live[u]["ob", half][:, pr * 2 : pr * 2 + 2, :]
+                nc.gpsimd.tensor_tensor(out=dst, in0=live[u]["raw", half, pr][:], in1=bias_f[:], op=ALU.add)
 
         def store(u, half):
             t_out = u * TB + half * 4
@@ -363,6 +377,7 @@ def tile_cfkanlayer_t_kernel(tc, x, cheby_coeffs, bias, out):
             "m0": lambda u: multiply(u, 0), "m1": lambda u: multiply(u, 1),
             "e00": lambda u: evac(u, 0, 0), "e01": lambda u: evac(u, 0, 1),
             "e10": lambda u: evac(u, 1, 0), "e11": lambda u: evac(u, 1, 1),
+            "a01": lambda u: add_bias(u, 0, 1), "a11": lambda u: add_bias(u, 1, 1),
             "st0": lambda u: store(u, 0), "st1": lambda u: store(u, 1),
             "d1": lambda u: send(u, 1), "d2": lambda u: send(u, 2), "d3": lambda u: send(u, 3), "d4": lambda u: send(u, 4),
             "d5": lambda u: send(u, 5), "d6": lambda u: send(u, 6), "d7": lambda u: send(u, 7),
@@ -371,13 +386,12 @@ def tile_cfkanlayer_t_kernel(tc, x, cheby_coeffs, bias, out):
         w_re = prepare_weights()
         tanh(0)
         turn(0)
-        w_codes = w_scales = bias_f = None
         for s in range(n_units):
             for name, lag in STEP:
                 u = s - lag
                 if 0 <= u < n_units:
                     OPS[name](u)
-                if s == W_STEP and name == W_AFTER:
-                    w_codes, w_scales, bias_f = turn_weights(w_re)
+                for w in W_AT.get((s, name), ()):
+                    W_OPS[w]()
         for name, u in TAIL:
             OPS[name](u)

from contextlib import ExitStack

import concourse.mybir as mybir
from concourse.masks import make_identity

F32 = mybir.dt.float32
BF16 = mybir.dt.bfloat16
U32 = mybir.dt.uint32
U8 = mybir.dt.uint8
FP8X4 = mybir.dt.float8_e4m3fn_x4
ACT = mybir.ActivationFunctionType
ALU = mybir.AluOpType

P = 128
N_ROWS, D_IN, N_OUT, N_DEG = 16384, 64, 256, 8
K_ALL = D_IN * N_DEG
FLOPS = 2 * N_ROWS * K_ALL * N_OUT

NB = N_ROWS // P
TB = 8
CH = P * 4
X_CHUNKS = (8, 24, 32, 64)
L2_BUFS = 5
LAG = 4
PLACE = (0, 1, 2, 3, 4, 5, 6, 7)
ACT_SENDS = ()
EARLY = 2
W_AT = {(0, "turn"): ("wt0", "wt1",), (1, "t5"): ("wc0",), (1, "p7"): ("wc1",), (2, "t5"): ("wq",), (2, "t7"): ("wb",)}
T3G = False
T6G = False
TAIL = (
    ("t3", 15),
    ("e10", 12),
    ("r6", 15),
    ("t5", 15),
    ("d5", 15),
    ("q0", 13),
    ("m0", 13),
    ("t3b", 15),
    ("d3", 15),
    ("p7", 15),
    ("q1", 13),
    ("e11", 12),
    ("a11", 12),
    ("m1", 13),
    ("t6", 15),
    ("d6", 15),
    ("t7", 15),
    ("d7", 15),
    ("st1", 12),
    ("q0", 14),
    ("e00", 13),
    ("e01", 13),
    ("m0", 14),
    ("st0", 13),
    ("q1", 14),
    ("e10", 13),
    ("e11", 13),
    ("a11", 13),
    ("m1", 14),
    ("st1", 13),
    ("e00", 14),
    ("q0", 15),
    ("e01", 14),
    ("a01", 14),
    ("m0", 15),
    ("st0", 14),
    ("q1", 15),
    ("e10", 14),
    ("e11", 14),
    ("a11", 14),
    ("m1", 15),
    ("st1", 14),
    ("e00", 15),
    ("e01", 15),
    ("st0", 15),
    ("e10", 15),
    ("e11", 15),
    ("st1", 15),
)
STEP = (
    ("tanh", -1),
    ("turn", -1),
    ("t3", 1),
    ("s4", 0),
    ("e10", 4),
    ("r6", 1),
    ("t5", 1),
    ("d5", 1),
    ("q", 0),
    ("q0", 3),
    ("m0", 3),
    ("t3b", 1),
    ("d3", 1),
    ("p7", 1),
    ("e11", 4),
    ("sq5", 0),
    ("q1", 3),
    ("m1", 3),
    ("a11", 4),
    ("t2", 0),
    ("t4", 0),
    ("t7", 1),
    ("d7", 1),
    ("t6", 1),
    ("st1", 4),
    ("t1", 0),
    ("d1", 0),
    ("d6", 1),
    ("e00", 3),
    ("d4", 0),
    ("e01", 3),
    ("d2", 0),
    ("st0", 3),
)


def ON_SCALAR(u, half, pr):
    return (half, pr) == (1, 1) and u < 14 or (half, pr, u) in ((0, 1, 14),)


def tile_cfkanlayer_t_kernel(tc, x, cheby_coeffs, bias, out):
    nc = tc.nc
    assert sum(X_CHUNKS) == NB
    with ExitStack() as ctx:
        const = ctx.enter_context(tc.tile_pool(name="const", bufs=1))
        work = ctx.enter_context(tc.tile_pool(name="work", bufs=3))
        cpool = ctx.enter_context(tc.tile_pool(name="cpool", bufs=4))
        outp = ctx.enter_context(tc.tile_pool(name="outp", bufs=4))
        tps = ctx.enter_context(tc.psum_pool(name="tps", bufs=4))
        ops = ctx.enter_context(tc.psum_pool(name="ops", bufs=4))

        ident = const.tile([P, P], F32, name="ident")
        make_identity(nc, ident[:])
        x_rows = x.rearrange("(p t) d -> p (t d)", t=NB)
        x_of_block = []

        def load_x(n_blocks):
            first = len(x_of_block)
            xt = const.tile([P, n_blocks * D_IN], BF16, name="x%d" % first)
            nc.sync.dma_start(out=xt[:], in_=x_rows[:, first * D_IN : (first + n_blocks) * D_IN])
            for j in range(n_blocks):
                x_of_block.append((xt, j))

        load_x(X_CHUNKS[0])
        w_raw = const.tile([P, 2, K_ALL], BF16, name="w_raw")
        nc.sync.dma_start(out=w_raw[:], in_=cheby_coeffs.rearrange("(h p) d k -> p h (d k)", p=P))
        for n_blocks in X_CHUNKS[1:]:
            load_x(n_blocks)

        shifts = const.tile([P, 3], F32, name="shifts")
        nc.vector.memset(shifts[:, 0:1], -2.0)
        nc.vector.memset(shifts[:, 1:2], -2.5)
        nc.vector.memset(shifts[:, 2:3], -1.0)
        bias_row = const.tile([P, N_OUT], BF16, name="bias_row")
        nc.vector.memset(bias_row[:], 0.0)
        nc.sync.dma_start(out=bias_row[0:1, :], in_=bias)
        ones = const.tile([P, CH], BF16, name="ones")
        nc.vector.memset(ones[:], 1.0)
        ident_bf = const.tile([P, P], BF16, name="ident_bf")
        nc.vector.tensor_copy(out=ident_bf[:], in_=ident[:])
        l2s = []
        for b in range(L2_BUFS):
            l2 = const.tile([P, TB * CH], BF16, name="l2_%d" % b, align_bytes=64)
            nc.sync.dma_start(out=l2[0:P:8, :], in_=ones[:])
            l2s.append(l2)

        out_rows = out.rearrange("(p t) o -> p t o", t=NB)

        def prepare_weights():
            w_re = const.tile([P, 2, K_ALL], BF16, name="w_re")
            w_dst = w_re[:].rearrange("p h (i g k) -> p h i g k", i=4, k=N_DEG)
            w_src = w_raw[:].rearrange("p h (g i k) -> p h i g k", i=4, k=N_DEG)
            for h in range(2):
                nc.vector.tensor_copy(out=w_dst[:, h], in_=w_src[:, h])
            return w_re

        w_grp = const.tile([P, N_OUT, 4], BF16, name="w_grp", align_bytes=64)
        w_codes = const.tile([P, N_OUT], U32, name="w_codes", align_bytes=64)
        w_scales = const.tile([P, N_OUT], U8, name="w_scales", align_bytes=64)
        bias_f = const.tile([P, 2, N_OUT], F32, name="bias_f")
        w_turned = {}

        def turn_weights(h):
            w_turned[h] = ops.tile([P, 4 * P], BF16, name="w_ps", tag="po")
            for i in range(4):
                nc.tensor.transpose(
                    out=w_turned[h][:, i * P : (i + 1) * P], in_=w_re[:, h, i * P : (i + 1) * P], identity=ident_bf[:]
                )

        def group_weights(h):
            nc.vector.tensor_copy(
                out=w_grp[:, h * P : (h + 1) * P, :], in_=w_turned[h][:].rearrange("p (i o) -> p o i", i=4)
            )

        def quantise_weights():
            nc.vector.quantize_mx(
                out=w_codes[:].bitcast(FP8X4), scales=w_scales[:], in_=w_grp[:].rearrange("p o a -> p (o a)")
            )

        def spread_bias():
            b_ps = ops.tile([P, N_OUT], F32, name="b_ps", tag="po")
            nc.tensor.matmul(out=b_ps[:], lhsT=ones[:, 0:P], rhs=bias_row[:], start=True, stop=True)
            for e in range(2):
                nc.vector.tensor_copy(out=bias_f[:, e, :], in_=b_ps[:])

        W_OPS = {
            "wt0": lambda: turn_weights(0), "wt1": lambda: turn_weights(1), "wc0": lambda: group_weights(0),
            "wc1": lambda: group_weights(1), "wq": quantise_weights, "wb": spread_bias,
        }
        live = {}
        n_units = NB // TB

        def by_row(tile):
            return tile[:].rearrange("q (p i) -> q p i", i=4)

        def new(u, key, dtype=F32):
            live[u][key] = work.tile([P, CH], dtype, name="w_%s" % key)
            return live[u][key]

        def send(u, k):
            eng = nc.scalar if k in ACT_SENDS else nc.sync
            eng.dma_start(out=l2s[u % L2_BUFS][PLACE[k] : P : 8, :], in_=live[u][k][:])

        def tanh(u):
            live[u] = {}
            new(u, "tr")
            xt, j = x_of_block[u * TB]
            nc.scalar.activation(
                out=live[u]["tr"][:].rearrange("p (i g t) -> p g t i", i=4, t=TB),
                in_=xt[:, j * D_IN : (j + TB) * D_IN].rearrange("p (t g i) -> p g t i", t=TB, i=4),
                func=ACT.Tanh,
            )

        def turn(u):
            ps = tps.tile([P, CH], F32, name="tp", tag="tp")
            for i in range(4):
                nc.tensor.transpose(
                    out=ps[:, i * P : (i + 1) * P], in_=live[u]["tr"][:, i * P : (i + 1) * P], identity=ident[:]
                )
            live[u]["t"] = ps[:].rearrange("q (i p) -> q p i", i=4)

        def s4(u):
            nc.scalar.activation(out=by_row(new(u, "s4")), in_=live[u]["t"], func=ACT.Square, scale=2.0)

        def q(u):
            nc.scalar.activation(out=new(u, "q")[:], in_=live[u]["s4"][:], func=ACT.Square, bias=shifts[:, 0:1])

        def sq5(u):
            nc.scalar.activation(out=new(u, "sq5")[:], in_=live[u]["s4"][:], func=ACT.Square, bias=shifts[:, 1:2])

        def t1(u):
            nc.scalar.copy(out=by_row(new(u, 1, BF16)), in_=live[u]["t"])

        def halved(u, k, src):
            nc.gpsimd.tensor_scalar(
                out=new(u, k, BF16)[:], in0=live[u][src][:], scalar1=0.5, scalar2=-1.0, op0=ALU.mult, op1=ALU.add
            )

        def t2(u):
            halved(u, 2, "s4")

        def t4(u):
            halved(u, 4, "q")

        def times_t(u, out_tile, src, shift):
            nc.vector.scalar_tensor_tensor(
                out=by_row(out_tile),
                in0=by_row(live[u][src]),
                scalar=shift,
                in1=live[u]["t"],
                op0=ALU.subtract,
                op1=ALU.mult,
            )

        def t3(u):
            times_t(u, new(u, "t3"), "s4", 3.0)

        def t5(u):
            times_t(u, new(u, 5, BF16), "sq5", 1.25)

        def r6(u):
            nc.scalar.activation(out=new(u, "r6")[:], in_=live[u]["t3"][:], func=ACT.Square)

        def t3b(u):
            dst = new(u, 3, BF16)[:]
            src = live[u]["t3"][:]
            if u < EARLY:
                nc.vector.tensor_copy(out=dst, in_=src)
            elif T3G:
                nc.gpsimd.tensor_scalar(out=dst, in0=src, scalar1=1.0, scalar2=0.0, op0=ALU.mult, op1=ALU.add)
            else:
                nc.scalar.copy(out=dst, in_=src)

        def t6(u):
            dst = new(u, 6, BF16)[:]
            src = live[u]["r6"][:]
            if u < EARLY or T6G:
                eng = nc.vector if u < EARLY else nc.gpsimd
                eng.tensor_scalar(out=dst, in0=src, scalar1=2.0, scalar2=-1.0, op0=ALU.mult, op1=ALU.add)
            else:
                nc.scalar.activation(out=dst, in_=src, func=ACT.Identity, scale=2.0, bias=shifts[:, 2:3])

        def p7(u):
            nc.vector.scalar_tensor_tensor(
                out=new(u, "p7")[:],
                in0=live[u]["q"][:],
                scalar=2.0,
                in1=live[u]["t3"][:],
                op0=ALU.subtract,
                op1=ALU.mult,
            )

        def t7(u):
            nc.vector.tensor_tensor(
                out=by_row(new(u, 7, BF16)), in0=by_row(live[u]["p7"]), in1=live[u]["t"], op=ALU.subtract
            )

        def quantise(u, half):
            cd = cpool.tile([P, 4 * P], U32, name="cod", align_bytes=64)
            sc = cpool.tile([P, 4 * P], U8, name="scl", align_bytes=64)
            live[u]["codes", half] = (cd, sc)
            nc.vector.quantize_mx(
                out=cd[:].bitcast(FP8X4),
                scales=sc[:],
                in_=l2s[u % L2_BUFS][:, half * 4 * CH : (half + 1) * 4 * CH],
            )

        def multiply(u, half):
            cd, sc = live[u]["codes", half]
            live[u]["ob", half] = outp.tile([P, 4, N_OUT], F32, name="ob")
            for pr in range(2):
                po = ops.tile([P, 2, N_OUT], F32, name="po", tag="po")
                live[u]["po", half, pr] = po
                for e in range(2):
                    b = pr * 2 + e
                    nc.tensor.matmul_mx(
                        out=po[:, e, :],
                        lhsT=cd[:, b * P : (b + 1) * P].bitcast(FP8X4),
                        lhsT_scale=sc[:, b * P : (b + 1) * P],
                        rhs=w_codes[:].bitcast(FP8X4),
                        rhs_scale=w_scales[:],
                        start=True,
                        stop=True,
                    )

        def evac(u, half, pr):
            dst = live[u]["ob", half][:, pr * 2 : pr * 2 + 2, :]
            po = live[u]["po", half, pr]
            if ON_SCALAR(u, half, pr):
                raw = outp.tile([P, 2, N_OUT], F32, name="raw")
                live[u]["raw", half, pr] = raw
                nc.scalar.copy(out=raw[:], in_=po[:])
            else:
                nc.vector.tensor_tensor(out=dst, in0=po[:], in1=bias_f[:], op=ALU.add)

        def add_bias(u, half, pr):
            if ON_SCALAR(u, half, pr):
                dst = live[u]["ob", half][:, pr * 2 : pr * 2 + 2, :]
                nc.gpsimd.tensor_tensor(out=dst, in0=live[u]["raw", half, pr][:], in1=bias_f[:], op=ALU.add)

        def store(u, half):
            t_out = u * TB + half * 4
            if u == n_units - 1 and half == 1:
                for pr in range(2):
                    nc.sync.dma_start(
                        out=out_rows[:, t_out + pr * 2 : t_out + pr * 2 + 2, :],
                        in_=live[u]["ob", half][:, pr * 2 : pr * 2 + 2, :],
                    )
            else:
                nc.sync.dma_start(out=out_rows[:, t_out : t_out + 4, :], in_=live[u]["ob", half][:])

        OPS = {
            "tanh": tanh, "turn": turn, "s4": s4, "q": q, "sq5": sq5, "t1": t1, "t2": t2, "t3": t3, "t3b": t3b, "t4": t4,
            "t5": t5, "r6": r6, "t6": t6, "p7": p7, "t7": t7,
            "q0": lambda u: quantise(u, 0), "q1": lambda u: quantise(u, 1),
            "m0": lambda u: multiply(u, 0), "m1": lambda u: multiply(u, 1),
            "e00": lambda u: evac(u, 0, 0), "e01": lambda u: evac(u, 0, 1),
            "e10": lambda u: evac(u, 1, 0), "e11": lambda u: evac(u, 1, 1),
            "a01": lambda u: add_bias(u, 0, 1), "a11": lambda u: add_bias(u, 1, 1),
            "st0": lambda u: store(u, 0), "st1": lambda u: store(u, 1),
            "d1": lambda u: send(u, 1), "d2": lambda u: send(u, 2), "d3": lambda u: send(u, 3), "d4": lambda u: send(u, 4),
            "d5": lambda u: send(u, 5), "d6": lambda u: send(u, 6), "d7": lambda u: send(u, 7),
        }
        ctx.enter_context(tc.manual_schedule())
        w_re = prepare_weights()
        tanh(0)
        turn(0)
        for s in range(n_units):
            for name, lag in STEP:
                u = s - lag
                if 0 <= u < n_units:
                    OPS[name](u)
                for w in W_AT.get((s, name), ()):
                    W_OPS[w]()
        for name, u in TAIL:
            OPS[name](u)
